import numpy as np
import ml_dtypes


def mxq(x, axis, fmt="e4m3"):
    dtype, down = {"e4m3": (ml_dtypes.float8_e4m3fn, 7), "e5m2": (ml_dtypes.float8_e5m2, 14)}[fmt]
    v = np.moveaxis(np.asarray(x, np.float32).astype(ml_dtypes.bfloat16).astype(np.float64), axis, -1)
    blocks = v.reshape(v.shape[:-1] + (-1, 32))
    amax = np.abs(blocks).max(-1, keepdims=True)
    byte = np.maximum(np.where(amax > 0, np.frexp(amax)[1] - 1 + 127, 0) - down, 1)
    scale = np.exp2(byte - 127.0)
    codes = (blocks / scale).astype(np.float32).astype(dtype).astype(np.float64)
    return np.moveaxis((codes * scale).reshape(v.shape), -1, axis)


WIDE = False


def mx_kscale(k):
    if not WIDE:
        return np.ones(k)
    levels = np.array([10, -10, 5, -5, 0])
    a = np.random.permutation(np.resize(levels, k // 512 * 4)).reshape(k // 512, 4)
    idx = np.arange(k)
    return np.exp2(a[idx // 512, idx % 128 // 32])


BF16 = ml_dtypes.bfloat16


def bf(x):
    return np.asarray(x, np.float32).astype(BF16)


def f64(x):
    return np.asarray(x).astype(np.float64)


B, S, D = 128, 1, 512


def sigmoid(v):
    return 1.0 / (1.0 + np.exp(-v))


def setup_inputs():
    s, t = mx_kscale(D), mx_kscale(D)
    return {
        "inputs": bf(np.random.standard_normal((B, D)) * s),
        "h_state": bf((np.random.standard_normal((B, S, D)) * 0.5 * t).reshape(B, S * D)),
        "c_state": bf(np.random.standard_normal((B, S * D)) * 0.5),
        "c_upd": bf(np.random.standard_normal((B, S, D))),
        "kernel": bf(np.random.standard_normal((D, 3 * D)) / np.sqrt(D) / s[:, None]),
        "recurrent_kernel": bf(np.random.standard_normal((D, 3 * D)) / np.sqrt(D) / t[:, None]),
        "bias": bf(np.random.standard_normal(3 * D) * 0.3),
    }


def reference(inputs, h_state, c_state, c_upd, kernel, recurrent_kernel, bias):
    h_tm1 = f64(h_state).reshape(B, S, D)
    c_tm1 = f64(c_state).reshape(B, S, D)
    xz = mxq(f64(inputs), 1, "e4m3") @ mxq(f64(kernel), 0, "e4m3")
    hz = mxq(h_tm1, 2, "e4m3") @ mxq(f64(recurrent_kernel), 0, "e4m3")
    z = xz[:, None, :] + hz + f64(bias)
    i = sigmoid(z[..., :D])
    f = sigmoid(z[..., D:2 * D])
    o = sigmoid(z[..., 2 * D:])
    c_new = f * c_tm1 + i * np.tanh(f64(c_upd))
    h_new = o * np.tanh(c_new)
    return h_new.reshape(B, -1), c_new.reshape(B, -1)

@@ -1,0 +1,180 @@
+from contextlib import ExitStack
+
+import concourse.mybir as mybir
+from concourse.masks import make_identity
+
+F32 = mybir.dt.float32
+BF16 = mybir.dt.bfloat16
+U32 = mybir.dt.uint32
+U8 = mybir.dt.uint8
+FP8X4 = mybir.dt.float8_e4m3fn_x4
+ACT = mybir.ActivationFunctionType
+
+P = 128
+PACK = 4
+D = 512
+GATES = 3
+OPERANDS = 2
+BLOCKS = D // P
+V_COLS = 192
+
+FLOPS = 2 * P * D * (GATES * D) * OPERANDS
+
+
+def tile_rlstmcell_pb_s_kernel(
+    tc, inputs, h_state, c_state, c_upd, kernel, recurrent_kernel, bias, out_0, out_1
+):
+    nc = tc.nc
+    weights = (kernel, recurrent_kernel)
+    chunks = [(g, a) for g in range(GATES) for a in range(OPERANDS)]
+
+    with ExitStack() as ctx:
+        consts = ctx.enter_context(tc.tile_pool(name="consts", bufs=1))
+        wpool = ctx.enter_context(tc.tile_pool(name="wpool", bufs=len(chunks)))
+        gpool = ctx.enter_context(tc.tile_pool(name="gpool", bufs=GATES))
+        psum_once = ctx.enter_context(tc.psum_pool(name="psum_once", bufs=1))
+        psum_gate = ctx.enter_context(tc.psum_pool(name="psum_gate", bufs=GATES))
+
+        bias_rows = consts.tile([P, P], BF16)
+        nc.vector.memset(bias_rows[:], 0.0)
+        nc.sync.dma_start(
+            out=bias_rows[0 : GATES * BLOCKS, :], in_=bias.rearrange("(r c) -> r c", c=P)
+        )
+
+        def load_chunk(g, a):
+            raw = wpool.tile([P, PACK, D], BF16)
+            nc.sync.dma_start(
+                out=raw[:],
+                in_=weights[a][:, g * D : (g + 1) * D].rearrange("(p j) n -> p j n", j=PACK),
+            )
+            return raw
+
+        raws = {}
+        raws[(0, 0)] = load_chunk(0, 0)
+        xh = consts.tile([P, OPERANDS, D], BF16)
+        nc.sync.dma_start(out=xh[:, 0, :], in_=inputs)
+        nc.sync.dma_start(out=xh[:, 1, :], in_=h_state)
+        raws[(0, 1)] = load_chunk(0, 1)
+        cu = consts.tile([P, D], BF16)
+        nc.sync.dma_start(out=cu[:], in_=c_upd.rearrange("b s d -> b (s d)"))
+        raws[(1, 0)] = load_chunk(1, 0)
+        c_old = consts.tile([P, D], BF16)
+        nc.sync.dma_start(out=c_old[:], in_=c_state)
+        raws[(1, 1)] = load_chunk(1, 1)
+        raws[(2, 0)] = load_chunk(2, 0)
+        raws[(2, 1)] = load_chunk(2, 1)
+
+        ident_f32 = consts.tile([P, P], F32)
+        make_identity(nc, ident_f32[:])
+        ident_bf = consts.tile([P, P], BF16)
+        make_identity(nc, ident_bf[:])
+        warm = consts.tile([P, 1], F32)
+        nc.vector.memset(warm[:], 0.0)
+        nc.scalar.activation(out=warm[:], in_=warm[:], func=ACT.Sigmoid)
+
+        bias_cols_ps = psum_once.tile([P, P], BF16)
+        nc.tensor.transpose(bias_cols_ps[:], bias_rows[:], ident_bf[:])
+        bias_cols = consts.tile([P, GATES * BLOCKS], BF16)
+        nc.vector.tensor_copy(out=bias_cols[:], in_=bias_cols_ps[:, 0 : GATES * BLOCKS])
+        bias_all = []
+        for g in range(GATES):
+            bias_ps = psum_gate.tile([P, D], BF16)
+            for q in range(BLOCKS):
+                r = g * BLOCKS + q
+                nc.tensor.transpose(
+                    bias_ps[:, q * P : (q + 1) * P],
+                    bias_cols[:, r : r + 1].to_broadcast([P, P]),
+                    ident_bf[:],
+                )
+            bias_sb = gpool.tile([P, D], BF16)
+            nc.scalar.copy(out=bias_sb[:], in_=bias_ps[:])
+            bias_all.append(bias_sb)
+
+        xh_words = xh[:].rearrange("b a k -> b (a k)").bitcast(F32).rearrange(
+            "b (a p u) -> b a u p", a=OPERANDS, u=2
+        )
+        xh_t = psum_once.tile([P, OPERANDS, 2, P], F32)
+        for a in range(OPERANDS):
+            for u in range(2):
+                nc.tensor.transpose(xh_t[:, a, u, :], xh_words[:, a, u, :], ident_f32[:])
+        xh_grouped = consts.tile([P, OPERANDS * P * PACK], BF16, align_bytes=64)
+        nc.vector.tensor_copy(
+            out=xh_grouped[:].bitcast(F32).rearrange("p (a b u) -> p a b u", a=OPERANDS, u=2),
+            in_=xh_t[:].rearrange("p a u b -> p a b u"),
+        )
+        xh_codes = consts.tile([P, OPERANDS * P], U32, align_bytes=64)
+        xh_scales = consts.tile([P, OPERANDS * P], U8, align_bytes=64)
+        nc.vector.quantize_mx(
+            out=xh_codes[:].bitcast(FP8X4), scales=xh_scales[:], in_=xh_grouped[:]
+        )
+
+        cand = consts.tile([P, D], F32)
+        nc.scalar.activation(out=cand[:], in_=cu[:], func=ACT.Tanh)
+
+        def regroup(g, a):
+            raw = raws[(g, a)]
+            grouped = wpool.tile([P, D, PACK], BF16, align_bytes=64)
+            nc.vector.tensor_copy(
+                out=grouped[:, 0:V_COLS, :].rearrange("p (c i) j -> p c j i", i=4),
+                in_=raw[:, :, 0:V_COLS].rearrange("p j (c i) -> p c j i", i=4),
+            )
+            nc.scalar.copy(
+                out=grouped[:, V_COLS:D, :].rearrange("p (c i) j -> p c j i", i=4),
+                in_=raw[:, :, V_COLS:D].rearrange("p j (c i) -> p c j i", i=4),
+            )
+            return grouped
+
+        def quantise(grouped):
+            codes = wpool.tile([P, D], U32, align_bytes=64)
+            scales = wpool.tile([P, D], U8, align_bytes=64)
+            nc.vector.quantize_mx(
+                out=codes[:].bitcast(FP8X4),
+                scales=scales[:],
+                in_=grouped[:].rearrange("p n j -> p (n j)"),
+            )
+            return codes, scales
+
+        def gate_value(g, z):
+            zb = gpool.tile([P, D], F32)
+            nc.vector.tensor_add(out=zb[:], in0=z[:], in1=bias_all[g][:])
+            gate = gpool.tile([P, D], F32)
+            nc.scalar.activation(out=gate[:], in_=zb[:], func=ACT.Sigmoid)
+            return gate
+
+        c_new = consts.tile([P, D], F32)
+        tanh_c = consts.tile([P, D], F32)
+        h_new = consts.tile([P, D], F32)
+        i_cand = consts.tile([P, D], F32)
+        f_c = consts.tile([P, D], F32)
+
+        grouped_next = regroup(*chunks[0])
+        z = None
+        for n, (g, a) in enumerate(chunks):
+            grouped = grouped_next
+            if n + 1 < len(chunks):
+                grouped_next = regroup(*chunks[n + 1])
+            codes, scales = quantise(grouped)
+            if a == 0:
+                z = psum_gate.tile([P, D], F32)
+            nc.tensor.matmul_mx(
+                out=z[:],
+                lhsT=xh_codes[:, a * P : (a + 1) * P].bitcast(FP8X4),
+                lhsT_scale=xh_scales[:, a * P : (a + 1) * P],
+                rhs=codes[:].bitcast(FP8X4),
+                rhs_scale=scales[:],
+                start=(a == 0),
+                stop=(a == OPERANDS - 1),
+            )
+            if a < OPERANDS - 1:
+                continue
+            gate = gate_value(g, z)
+            if g == 0:
+                nc.vector.tensor_mul(out=i_cand[:], in0=gate[:], in1=cand[:])
+            elif g == 1:
+                nc.vector.tensor_mul(out=f_c[:], in0=gate[:], in1=c_old[:])
+                nc.vector.tensor_add(out=c_new[:], in0=f_c[:], in1=i_cand[:])
+                nc.sync.dma_start(out=out_1, in_=c_new[:])
+                nc.scalar.activation(out=tanh_c[:], in_=c_new[:], func=ACT.Tanh)
+            else:
+                nc.vector.tensor_mul(out=h_new[:], in0=gate[:], in1=tanh_c[:])
+                nc.sync.dma_start(out=out_0, in_=h_new[:])

@@ -16,7 +16,8 @@ D = 512
 GATES = 3
 OPERANDS = 2
 BLOCKS = D // P
-V_COLS = 192
+PIECE = 256
+PIECES = D // PIECE
 
 FLOPS = 2 * P * D * (GATES * D) * OPERANDS
 
@@ -26,43 +27,41 @@ def tile_rlstmcell_pb_s_kernel(
 ):
     nc = tc.nc
     weights = (kernel, recurrent_kernel)
-    chunks = [(g, a) for g in range(GATES) for a in range(OPERANDS)]
+    pieces = [(g, s * PIECE) for g in range(GATES) for s in range(PIECES)]
 
     with ExitStack() as ctx:
         consts = ctx.enter_context(tc.tile_pool(name="consts", bufs=1))
-        wpool = ctx.enter_context(tc.tile_pool(name="wpool", bufs=len(chunks)))
-        gpool = ctx.enter_context(tc.tile_pool(name="gpool", bufs=GATES))
+        wpool = ctx.enter_context(tc.tile_pool(name="wpool", bufs=len(pieces)))
         psum_once = ctx.enter_context(tc.psum_pool(name="psum_once", bufs=1))
         psum_gate = ctx.enter_context(tc.psum_pool(name="psum_gate", bufs=GATES))
 
+        def load_piece(g, first):
+            raw = wpool.tile([P, OPERANDS, PACK, PIECE], BF16)
+            for a in range(OPERANDS):
+                nc.sync.dma_start(
+                    out=raw[:, a, :, :],
+                    in_=weights[a][:, g * D + first : g * D + first + PIECE].rearrange(
+                        "(p j) n -> p j n", j=PACK
+                    ),
+                )
+            return raw
+
+        raws = [load_piece(*pieces[0])]
         bias_rows = consts.tile([P, P], BF16)
         nc.vector.memset(bias_rows[:], 0.0)
         nc.sync.dma_start(
             out=bias_rows[0 : GATES * BLOCKS, :], in_=bias.rearrange("(r c) -> r c", c=P)
         )
-
-        def load_chunk(g, a):
-            raw = wpool.tile([P, PACK, D], BF16)
-            nc.sync.dma_start(
-                out=raw[:],
-                in_=weights[a][:, g * D : (g + 1) * D].rearrange("(p j) n -> p j n", j=PACK),
-            )
-            return raw
-
-        raws = {}
-        raws[(0, 0)] = load_chunk(0, 0)
         xh = consts.tile([P, OPERANDS, D], BF16)
         nc.sync.dma_start(out=xh[:, 0, :], in_=inputs)
         nc.sync.dma_start(out=xh[:, 1, :], in_=h_state)
-        raws[(0, 1)] = load_chunk(0, 1)
         cu = consts.tile([P, D], BF16)
         nc.sync.dma_start(out=cu[:], in_=c_upd.rearrange("b s d -> b (s d)"))
-        raws[(1, 0)] = load_chunk(1, 0)
+        raws.append(load_piece(*pieces[1]))
         c_old = consts.tile([P, D], BF16)
         nc.sync.dma_start(out=c_old[:], in_=c_state)
-        raws[(1, 1)] = load_chunk(1, 1)
-        raws[(2, 0)] = load_chunk(2, 0)
-        raws[(2, 1)] = load_chunk(2, 1)
+        for piece in pieces[2:]:
+            raws.append(load_piece(*piece))
 
         ident_f32 = consts.tile([P, P], F32)
         make_identity(nc, ident_f32[:])
@@ -86,7 +85,7 @@ def tile_rlstmcell_pb_s_kernel(
                     bias_cols[:, r : r + 1].to_broadcast([P, P]),
                     ident_bf[:],
                 )
-            bias_sb = gpool.tile([P, D], BF16)
+            bias_sb = consts.tile([P, D], BF16, name="bias_sb%d" % g)
             nc.scalar.copy(out=bias_sb[:], in_=bias_ps[:])
             bias_all.append(bias_sb)
 
@@ -111,35 +110,17 @@ def tile_rlstmcell_pb_s_kernel(
         cand = consts.tile([P, D], F32)
         nc.scalar.activation(out=cand[:], in_=cu[:], func=ACT.Tanh)
 
-        def regroup(g, a):
-            raw = raws[(g, a)]
-            grouped = wpool.tile([P, D, PACK], BF16, align_bytes=64)
+        def regroup(raw):
+            grouped = wpool.tile([P, OPERANDS, PIECE, PACK], BF16, align_bytes=64)
             nc.vector.tensor_copy(
-                out=grouped[:, 0:V_COLS, :].rearrange("p (c i) j -> p c j i", i=4),
-                in_=raw[:, :, 0:V_COLS].rearrange("p j (c i) -> p c j i", i=4),
+                out=grouped[:, 0, :, :].rearrange("p (c i) j -> p c j i", i=4),
+                in_=raw[:, 0, :, :].rearrange("p j (c i) -> p c j i", i=4),
             )
             nc.scalar.copy(
-                out=grouped[:, V_COLS:D, :].rearrange("p (c i) j -> p c j i", i=4),
-                in_=raw[:, :, V_COLS:D].rearrange("p j (c i) -> p c j i", i=4),
+                out=grouped[:, 1, :, :].rearrange("p (c i) j -> p c j i", i=4),
+                in_=raw[:, 1, :, :].rearrange("p j (c i) -> p c j i", i=4),
             )
             return grouped
-
-        def quantise(grouped):
-            codes = wpool.tile([P, D], U32, align_bytes=64)
-            scales = wpool.tile([P, D], U8, align_bytes=64)
-            nc.vector.quantize_mx(
-                out=codes[:].bitcast(FP8X4),
-                scales=scales[:],
-                in_=grouped[:].rearrange("p n j -> p (n j)"),
-            )
-            return codes, scales
-
-        def gate_value(g, z):
-            zb = gpool.tile([P, D], F32)
-            nc.vector.tensor_add(out=zb[:], in0=z[:], in1=bias_all[g][:])
-            gate = gpool.tile([P, D], F32)
-            nc.scalar.activation(out=gate[:], in_=zb[:], func=ACT.Sigmoid)
-            return gate
 
         c_new = consts.tile([P, D], F32)
         tanh_c = consts.tile([P, D], F32)
@@ -147,34 +128,43 @@ def tile_rlstmcell_pb_s_kernel(
         i_cand = consts.tile([P, D], F32)
         f_c = consts.tile([P, D], F32)
 
-        grouped_next = regroup(*chunks[0])
-        z = None
-        for n, (g, a) in enumerate(chunks):
-            grouped = grouped_next
-            if n + 1 < len(chunks):
-                grouped_next = regroup(*chunks[n + 1])
-            codes, scales = quantise(grouped)
-            if a == 0:
-                z = psum_gate.tile([P, D], F32)
-            nc.tensor.matmul_mx(
-                out=z[:],
-                lhsT=xh_codes[:, a * P : (a + 1) * P].bitcast(FP8X4),
-                lhsT_scale=xh_scales[:, a * P : (a + 1) * P],
-                rhs=codes[:].bitcast(FP8X4),
-                rhs_scale=scales[:],
-                start=(a == 0),
-                stop=(a == OPERANDS - 1),
-            )
-            if a < OPERANDS - 1:
-                continue
-            gate = gate_value(g, z)
+        def finish_piece(g, cols, z):
+            zb = wpool.tile([P, PIECE], F32)
+            nc.vector.tensor_add(out=zb[:], in0=z[:], in1=bias_all[g][:, cols])
+            gate = wpool.tile([P, PIECE], F32)
+            nc.scalar.activation(out=gate[:], in_=zb[:], func=ACT.Sigmoid)
             if g == 0:
-                nc.vector.tensor_mul(out=i_cand[:], in0=gate[:], in1=cand[:])
+                nc.vector.tensor_mul(out=i_cand[:, cols], in0=gate[:], in1=cand[:, cols])
             elif g == 1:
-                nc.vector.tensor_mul(out=f_c[:], in0=gate[:], in1=c_old[:])
-                nc.vector.tensor_add(out=c_new[:], in0=f_c[:], in1=i_cand[:])
-                nc.sync.dma_start(out=out_1, in_=c_new[:])
-                nc.scalar.activation(out=tanh_c[:], in_=c_new[:], func=ACT.Tanh)
+                nc.vector.tensor_mul(out=f_c[:, cols], in0=gate[:], in1=c_old[:, cols])
+                nc.vector.tensor_add(out=c_new[:, cols], in0=f_c[:, cols], in1=i_cand[:, cols])
+                nc.sync.dma_start(out=out_1[:, cols], in_=c_new[:, cols])
+                nc.scalar.activation(out=tanh_c[:, cols], in_=c_new[:, cols], func=ACT.Tanh)
             else:
-                nc.vector.tensor_mul(out=h_new[:], in0=gate[:], in1=tanh_c[:])
-                nc.sync.dma_start(out=out_0, in_=h_new[:])
+                nc.vector.tensor_mul(out=h_new[:, cols], in0=gate[:], in1=tanh_c[:, cols])
+                nc.sync.dma_start(out=out_0[:, cols], in_=h_new[:, cols])
+
+        grouped_next = regroup(raws[0])
+        for m, (g, first) in enumerate(pieces):
+            grouped = grouped_next
+            if m + 1 < len(pieces):
+                grouped_next = regroup(raws[m + 1])
+            codes = wpool.tile([P, OPERANDS, PIECE], U32, align_bytes=64)
+            scales = wpool.tile([P, OPERANDS, PIECE], U8, align_bytes=64)
+            nc.vector.quantize_mx(
+                out=codes[:].rearrange("p a n -> p (a n)").bitcast(FP8X4),
+                scales=scales[:].rearrange("p a n -> p (a n)"),
+                in_=grouped[:].rearrange("p a n j -> p (a n j)"),
+            )
+            z = psum_gate.tile([P, PIECE], F32)
+            for a in range(OPERANDS):
+                nc.tensor.matmul_mx(
+                    out=z[:],
+                    lhsT=xh_codes[:, a * P : (a + 1) * P].bitcast(FP8X4),
+                    lhsT_scale=xh_scales[:, a * P : (a + 1) * P],
+                    rhs=codes[:, a, :].bitcast(FP8X4),
+                    rhs_scale=scales[:, a, :],
+                    start=(a == 0),
+                    stop=(a == OPERANDS - 1),
+                )
+            finish_piece(g, slice(first, first + PIECE), z)

@@ -31,37 +31,41 @@ def tile_rlstmcell_pb_s_kernel(
 
     with ExitStack() as ctx:
         consts = ctx.enter_context(tc.tile_pool(name="consts", bufs=1))
+        gpool = ctx.enter_context(tc.tile_pool(name="gpool", bufs=GATES))
         wpool = ctx.enter_context(tc.tile_pool(name="wpool", bufs=len(pieces)))
         psum_once = ctx.enter_context(tc.psum_pool(name="psum_once", bufs=1))
         psum_gate = ctx.enter_context(tc.psum_pool(name="psum_gate", bufs=GATES))
 
-        def load_piece(g, first):
-            raw = wpool.tile([P, OPERANDS, PACK, PIECE], BF16)
+        raws = []
+        for g in range(GATES):
+            raws.append(gpool.tile([P, OPERANDS, PACK, D], BF16, name="raw"))
+
+        def load_weights(g, first, width):
             for a in range(OPERANDS):
                 nc.sync.dma_start(
-                    out=raw[:, a, :, :],
-                    in_=weights[a][:, g * D + first : g * D + first + PIECE].rearrange(
+                    out=raws[g][:, a, :, first : first + width],
+                    in_=weights[a][:, g * D + first : g * D + first + width].rearrange(
                         "(p j) n -> p j n", j=PACK
                     ),
                 )
-            return raw
 
-        raws = [load_piece(*pieces[0])]
+        load_weights(0, 0, PIECE)
+        xh = consts.tile([P, OPERANDS, D], BF16)
+        nc.sync.dma_start(out=xh[:, 0, :], in_=inputs)
+        nc.sync.dma_start(out=xh[:, 1, :], in_=h_state)
         bias_rows = consts.tile([P, P], BF16)
         nc.vector.memset(bias_rows[:], 0.0)
         nc.sync.dma_start(
             out=bias_rows[0 : GATES * BLOCKS, :], in_=bias.rearrange("(r c) -> r c", c=P)
         )
-        xh = consts.tile([P, OPERANDS, D], BF16)
-        nc.sync.dma_start(out=xh[:, 0, :], in_=inputs)
-        nc.sync.dma_start(out=xh[:, 1, :], in_=h_state)
+        for s in range(1, PIECES):
+            load_weights(0, s * PIECE, PIECE)
         cu = consts.tile([P, D], BF16)
         nc.sync.dma_start(out=cu[:], in_=c_upd.rearrange("b s d -> b (s d)"))
-        raws.append(load_piece(*pieces[1]))
+        load_weights(1, 0, D)
         c_old = consts.tile([P, D], BF16)
         nc.sync.dma_start(out=c_old[:], in_=c_state)
-        for piece in pieces[2:]:
-            raws.append(load_piece(*piece))
+        load_weights(2, 0, D)
 
         ident_f32 = consts.tile([P, P], F32)
         make_identity(nc, ident_f32[:])
@@ -97,7 +101,7 @@ def tile_rlstmcell_pb_s_kernel(
             for u in range(2):
                 nc.tensor.transpose(xh_t[:, a, u, :], xh_words[:, a, u, :], ident_f32[:])
         xh_grouped = consts.tile([P, OPERANDS * P * PACK], BF16, align_bytes=64)
-        nc.vector.tensor_copy(
+        nc.scalar.copy(
             out=xh_grouped[:].bitcast(F32).rearrange("p (a b u) -> p a b u", a=OPERANDS, u=2),
             in_=xh_t[:].rearrange("p a u b -> p a b u"),
         )
@@ -110,15 +114,16 @@ def tile_rlstmcell_pb_s_kernel(
         cand = consts.tile([P, D], F32)
         nc.scalar.activation(out=cand[:], in_=cu[:], func=ACT.Tanh)
 
-        def regroup(raw):
+        def regroup(g, first):
+            cols = slice(first, first + PIECE)
             grouped = wpool.tile([P, OPERANDS, PIECE, PACK], BF16, align_bytes=64)
-            nc.vector.tensor_copy(
-                out=grouped[:, 0, :, :].rearrange("p (c i) j -> p c j i", i=4),
-                in_=raw[:, 0, :, :].rearrange("p j (c i) -> p c j i", i=4),
-            )
             nc.scalar.copy(
+                out=grouped[:, 0, :, :].rearrange("p (c i) j -> p c j i", i=4),
+                in_=raws[g][:, 0, :, cols].rearrange("p j (c i) -> p c j i", i=4),
+            )
+            nc.vector.tensor_copy(
                 out=grouped[:, 1, :, :].rearrange("p (c i) j -> p c j i", i=4),
-                in_=raw[:, 1, :, :].rearrange("p j (c i) -> p c j i", i=4),
+                in_=raws[g][:, 1, :, cols].rearrange("p j (c i) -> p c j i", i=4),
             )
             return grouped
 
@@ -144,11 +149,11 @@ def tile_rlstmcell_pb_s_kernel(
                 nc.vector.tensor_mul(out=h_new[:, cols], in0=gate[:], in1=tanh_c[:, cols])
                 nc.sync.dma_start(out=out_0[:, cols], in_=h_new[:, cols])
 
-        grouped_next = regroup(raws[0])
+        grouped_next = regroup(*pieces[0])
         for m, (g, first) in enumerate(pieces):
             grouped = grouped_next
             if m + 1 < len(pieces):
-                grouped_next = regroup(raws[m + 1])
+                grouped_next = regroup(*pieces[m + 1])
             codes = wpool.tile([P, OPERANDS, PIECE], U32, align_bytes=64)
             scales = wpool.tile([P, OPERANDS, PIECE], U8, align_bytes=64)
             nc.vector.quantize_mx(

@@ -18,6 +18,7 @@ OPERANDS = 2
 BLOCKS = D // P
 PIECE = 256
 PIECES = D // PIECE
+PIECE_BLOCKS = PIECE // P
 
 FLOPS = 2 * P * D * (GATES * D) * OPERANDS
 
@@ -31,41 +32,37 @@ def tile_rlstmcell_pb_s_kernel(
 
     with ExitStack() as ctx:
         consts = ctx.enter_context(tc.tile_pool(name="consts", bufs=1))
-        gpool = ctx.enter_context(tc.tile_pool(name="gpool", bufs=GATES))
         wpool = ctx.enter_context(tc.tile_pool(name="wpool", bufs=len(pieces)))
-        psum_once = ctx.enter_context(tc.psum_pool(name="psum_once", bufs=1))
-        psum_gate = ctx.enter_context(tc.psum_pool(name="psum_gate", bufs=GATES))
+        psum_in = ctx.enter_context(tc.psum_pool(name="psum_in", bufs=1))
+        psum_gate = ctx.enter_context(tc.psum_pool(name="psum_gate", bufs=3))
+        psum_out = ctx.enter_context(tc.psum_pool(name="psum_out", bufs=2))
 
-        raws = []
-        for g in range(GATES):
-            raws.append(gpool.tile([P, OPERANDS, PACK, D], BF16, name="raw"))
-
-        def load_weights(g, first, width):
+        def load_piece(g, first):
+            raw = wpool.tile([P, OPERANDS, PACK, PIECE], BF16)
             for a in range(OPERANDS):
                 nc.sync.dma_start(
-                    out=raws[g][:, a, :, first : first + width],
-                    in_=weights[a][:, g * D + first : g * D + first + width].rearrange(
+                    out=raw[:, a, :, :],
+                    in_=weights[a][:, g * D + first : g * D + first + PIECE].rearrange(
                         "(p j) n -> p j n", j=PACK
                     ),
                 )
+            return raw
 
-        load_weights(0, 0, PIECE)
-        xh = consts.tile([P, OPERANDS, D], BF16)
-        nc.sync.dma_start(out=xh[:, 0, :], in_=inputs)
-        nc.sync.dma_start(out=xh[:, 1, :], in_=h_state)
+        raws = [load_piece(*pieces[0])]
         bias_rows = consts.tile([P, P], BF16)
         nc.vector.memset(bias_rows[:], 0.0)
         nc.sync.dma_start(
             out=bias_rows[0 : GATES * BLOCKS, :], in_=bias.rearrange("(r c) -> r c", c=P)
         )
-        for s in range(1, PIECES):
-            load_weights(0, s * PIECE, PIECE)
-        cu = consts.tile([P, D], BF16)
-        nc.sync.dma_start(out=cu[:], in_=c_upd.rearrange("b s d -> b (s d)"))
-        load_weights(1, 0, D)
-        c_old = consts.tile([P, D], BF16)
-        nc.sync.dma_start(out=c_old[:], in_=c_state)
-        load_weights(2, 0, D)
+        xh = consts.tile([P, OPERANDS, D], BF16)
+        nc.sync.dma_start(out=xh[:, 0, :], in_=inputs)
+        nc.sync.dma_start(out=xh[:, 1, :], in_=h_state)
+        cell_in = consts.tile([P, 2, D], BF16)
+        nc.sync.dma_start(out=cell_in[:, 0, :], in_=c_upd.rearrange("b s d -> b (s d)"))
+        raws.append(load_piece(*pieces[1]))
+        nc.sync.dma_start(out=cell_in[:, 1, :], in_=c_state)
+        for piece in pieces[2:]:
+            raws.append(load_piece(*piece))
 
         ident_f32 = consts.tile([P, P], F32)
         make_identity(nc, ident_f32[:])
@@ -75,33 +72,20 @@ def tile_rlstmcell_pb_s_kernel(
         nc.vector.memset(warm[:], 0.0)
         nc.scalar.activation(out=warm[:], in_=warm[:], func=ACT.Sigmoid)
 
-        bias_cols_ps = psum_once.tile([P, P], BF16)
+        bias_cols_ps = psum_in.tile([P, P], BF16)
         nc.tensor.transpose(bias_cols_ps[:], bias_rows[:], ident_bf[:])
-        bias_cols = consts.tile([P, GATES * BLOCKS], BF16)
+        bias_cols = consts.tile([P, GATES * BLOCKS], F32)
         nc.vector.tensor_copy(out=bias_cols[:], in_=bias_cols_ps[:, 0 : GATES * BLOCKS])
-        bias_all = []
-        for g in range(GATES):
-            bias_ps = psum_gate.tile([P, D], BF16)
-            for q in range(BLOCKS):
-                r = g * BLOCKS + q
-                nc.tensor.transpose(
-                    bias_ps[:, q * P : (q + 1) * P],
-                    bias_cols[:, r : r + 1].to_broadcast([P, P]),
-                    ident_bf[:],
-                )
-            bias_sb = consts.tile([P, D], BF16, name="bias_sb%d" % g)
-            nc.scalar.copy(out=bias_sb[:], in_=bias_ps[:])
-            bias_all.append(bias_sb)
 
         xh_words = xh[:].rearrange("b a k -> b (a k)").bitcast(F32).rearrange(
             "b (a p u) -> b a u p", a=OPERANDS, u=2
         )
-        xh_t = psum_once.tile([P, OPERANDS, 2, P], F32)
+        xh_t = psum_in.tile([P, OPERANDS, 2, P], F32)
         for a in range(OPERANDS):
             for u in range(2):
                 nc.tensor.transpose(xh_t[:, a, u, :], xh_words[:, a, u, :], ident_f32[:])
         xh_grouped = consts.tile([P, OPERANDS * P * PACK], BF16, align_bytes=64)
-        nc.scalar.copy(
+        nc.vector.tensor_copy(
             out=xh_grouped[:].bitcast(F32).rearrange("p (a b u) -> p a b u", a=OPERANDS, u=2),
             in_=xh_t[:].rearrange("p a u b -> p a b u"),
         )
@@ -111,19 +95,23 @@ def tile_rlstmcell_pb_s_kernel(
             out=xh_codes[:].bitcast(FP8X4), scales=xh_scales[:], in_=xh_grouped[:]
         )
 
+        cell_t = psum_in.tile([P, 2, D], BF16)
+        for t in range(2):
+            for q in range(BLOCKS):
+                block = slice(q * P, (q + 1) * P)
+                nc.tensor.transpose(cell_t[:, t, block], cell_in[:, t, block], ident_bf[:])
         cand = consts.tile([P, D], F32)
-        nc.scalar.activation(out=cand[:], in_=cu[:], func=ACT.Tanh)
+        nc.scalar.activation(out=cand[:], in_=cell_t[:, 0, :], func=ACT.Tanh)
 
-        def regroup(g, first):
-            cols = slice(first, first + PIECE)
+        def regroup(raw):
             grouped = wpool.tile([P, OPERANDS, PIECE, PACK], BF16, align_bytes=64)
-            nc.scalar.copy(
-                out=grouped[:, 0, :, :].rearrange("p (c i) j -> p c j i", i=4),
-                in_=raws[g][:, 0, :, cols].rearrange("p j (c i) -> p c j i", i=4),
-            )
             nc.vector.tensor_copy(
+                out=grouped[:, 0, :, :].rearrange("p (c i) j -> p c j i", i=4),
+                in_=raw[:, 0, :, :].rearrange("p j (c i) -> p c j i", i=4),
+            )
+            nc.scalar.copy(
                 out=grouped[:, 1, :, :].rearrange("p (c i) j -> p c j i", i=4),
-                in_=raws[g][:, 1, :, cols].rearrange("p j (c i) -> p c j i", i=4),
+                in_=raw[:, 1, :, :].rearrange("p j (c i) -> p c j i", i=4),
             )
             return grouped
 
@@ -133,27 +121,45 @@ def tile_rlstmcell_pb_s_kernel(
         i_cand = consts.tile([P, D], F32)
         f_c = consts.tile([P, D], F32)
 
-        def finish_piece(g, cols, z):
-            zb = wpool.tile([P, PIECE], F32)
-            nc.vector.tensor_add(out=zb[:], in0=z[:], in1=bias_all[g][:, cols])
+        def store_piece(out, value, first, copy):
+            back = psum_out.tile([P, PIECE], F32)
+            for q in range(PIECE_BLOCKS):
+                nc.tensor.transpose(
+                    back[:, q * P : (q + 1) * P],
+                    value[:, first + q * P : first + (q + 1) * P],
+                    ident_f32[:],
+                )
+            rows = wpool.tile([P, PIECE], F32)
+            copy(out=rows[:], in_=back[:])
+            nc.sync.dma_start(out=out[:, first : first + PIECE], in_=rows[:])
+
+        def finish_piece(g, first, z):
+            cols = slice(first, first + PIECE)
             gate = wpool.tile([P, PIECE], F32)
-            nc.scalar.activation(out=gate[:], in_=zb[:], func=ACT.Sigmoid)
+            for q in range(PIECE_BLOCKS):
+                r = g * BLOCKS + first // P + q
+                nc.scalar.activation(
+                    out=gate[:, q * P : (q + 1) * P],
+                    in_=z[:, q * P : (q + 1) * P],
+                    func=ACT.Sigmoid,
+                    bias=bias_cols[:, r : r + 1],
+                )
             if g == 0:
                 nc.vector.tensor_mul(out=i_cand[:, cols], in0=gate[:], in1=cand[:, cols])
             elif g == 1:
-                nc.vector.tensor_mul(out=f_c[:, cols], in0=gate[:], in1=c_old[:, cols])
+                nc.vector.tensor_mul(out=f_c[:, cols], in0=gate[:], in1=cell_t[:, 1, cols])
                 nc.vector.tensor_add(out=c_new[:, cols], in0=f_c[:, cols], in1=i_cand[:, cols])
-                nc.sync.dma_start(out=out_1[:, cols], in_=c_new[:, cols])
                 nc.scalar.activation(out=tanh_c[:, cols], in_=c_new[:, cols], func=ACT.Tanh)
+                store_piece(out_1, c_new, first, nc.vector.tensor_copy)
             else:
                 nc.vector.tensor_mul(out=h_new[:, cols], in0=gate[:], in1=tanh_c[:, cols])
-                nc.sync.dma_start(out=out_0[:, cols], in_=h_new[:, cols])
+                store_piece(out_0, h_new, first, nc.scalar.copy)
 
-        grouped_next = regroup(*pieces[0])
+        grouped_next = regroup(raws[0])
         for m, (g, first) in enumerate(pieces):
             grouped = grouped_next
             if m + 1 < len(pieces):
-                grouped_next = regroup(*pieces[m + 1])
+                grouped_next = regroup(raws[m + 1])
             codes = wpool.tile([P, OPERANDS, PIECE], U32, align_bytes=64)
             scales = wpool.tile([P, OPERANDS, PIECE], U8, align_bytes=64)
             nc.vector.quantize_mx(
@@ -162,14 +168,16 @@ def tile_rlstmcell_pb_s_kernel(
                 in_=grouped[:].rearrange("p a n j -> p (a n j)"),
             )
             z = psum_gate.tile([P, PIECE], F32)
-            for a in range(OPERANDS):
-                nc.tensor.matmul_mx(
-                    out=z[:],
-                    lhsT=xh_codes[:, a * P : (a + 1) * P].bitcast(FP8X4),
-                    lhsT_scale=xh_scales[:, a * P : (a + 1) * P],
-                    rhs=codes[:, a, :].bitcast(FP8X4),
-                    rhs_scale=scales[:, a, :],
-                    start=(a == 0),
-                    stop=(a == OPERANDS - 1),
-                )
-            finish_piece(g, slice(first, first + PIECE), z)
+            for q in range(PIECE_BLOCKS):
+                block = slice(q * P, (q + 1) * P)
+                for a in range(OPERANDS):
+                    nc.tensor.matmul_mx(
+                        out=z[:, block],
+                        lhsT=codes[:, a, block].bitcast(FP8X4),
+                        lhsT_scale=scales[:, a, block],
+                        rhs=xh_codes[:, a * P : (a + 1) * P].bitcast(FP8X4),
+                        rhs_scale=xh_scales[:, a * P : (a + 1) * P],
+                        start=(a == 0),
+                        stop=(a == OPERANDS - 1),
+                    )
+            finish_piece(g, first, z)

@@ -35,7 +35,7 @@ def tile_rlstmcell_pb_s_kernel(
         wpool = ctx.enter_context(tc.tile_pool(name="wpool", bufs=len(pieces)))
         psum_in = ctx.enter_context(tc.psum_pool(name="psum_in", bufs=1))
         psum_gate = ctx.enter_context(tc.psum_pool(name="psum_gate", bufs=3))
-        psum_out = ctx.enter_context(tc.psum_pool(name="psum_out", bufs=2))
+        psum_out = ctx.enter_context(tc.psum_pool(name="psum_out", bufs=3))
 
         def load_piece(g, first):
             raw = wpool.tile([P, OPERANDS, PACK, PIECE], BF16)
@@ -48,7 +48,7 @@ def tile_rlstmcell_pb_s_kernel(
                 )
             return raw
 
-        raws = [load_piece(*pieces[0])]
+        raws = [load_piece(*pieces[0]), load_piece(*pieces[1])]
         bias_rows = consts.tile([P, P], BF16)
         nc.vector.memset(bias_rows[:], 0.0)
         nc.sync.dma_start(
@@ -59,9 +59,9 @@ def tile_rlstmcell_pb_s_kernel(
         nc.sync.dma_start(out=xh[:, 1, :], in_=h_state)
         cell_in = consts.tile([P, 2, D], BF16)
         nc.sync.dma_start(out=cell_in[:, 0, :], in_=c_upd.rearrange("b s d -> b (s d)"))
-        raws.append(load_piece(*pieces[1]))
+        raws.append(load_piece(*pieces[2]))
         nc.sync.dma_start(out=cell_in[:, 1, :], in_=c_state)
-        for piece in pieces[2:]:
+        for piece in pieces[3:]:
             raws.append(load_piece(*piece))
 
         ident_f32 = consts.tile([P, P], F32)
@@ -95,13 +95,8 @@ def tile_rlstmcell_pb_s_kernel(
             out=xh_codes[:].bitcast(FP8X4), scales=xh_scales[:], in_=xh_grouped[:]
         )
 
-        cell_t = psum_in.tile([P, 2, D], BF16)
-        for t in range(2):
-            for q in range(BLOCKS):
-                block = slice(q * P, (q + 1) * P)
-                nc.tensor.transpose(cell_t[:, t, block], cell_in[:, t, block], ident_bf[:])
         cand = consts.tile([P, D], F32)
-        nc.scalar.activation(out=cand[:], in_=cell_t[:, 0, :], func=ACT.Tanh)
+        nc.scalar.activation(out=cand[:], in_=cell_in[:, 0, :], func=ACT.Tanh)
 
         def regroup(raw):
             grouped = wpool.tile([P, OPERANDS, PIECE, PACK], BF16, align_bytes=64)
@@ -121,39 +116,31 @@ def tile_rlstmcell_pb_s_kernel(
         i_cand = consts.tile([P, D], F32)
         f_c = consts.tile([P, D], F32)
 
-        def store_piece(out, value, first, copy):
-            back = psum_out.tile([P, PIECE], F32)
-            for q in range(PIECE_BLOCKS):
-                nc.tensor.transpose(
-                    back[:, q * P : (q + 1) * P],
-                    value[:, first + q * P : first + (q + 1) * P],
-                    ident_f32[:],
-                )
-            rows = wpool.tile([P, PIECE], F32)
-            copy(out=rows[:], in_=back[:])
-            nc.sync.dma_start(out=out[:, first : first + PIECE], in_=rows[:])
-
         def finish_piece(g, first, z):
             cols = slice(first, first + PIECE)
-            gate = wpool.tile([P, PIECE], F32)
+            gate_t = wpool.tile([P, PIECE], F32)
             for q in range(PIECE_BLOCKS):
                 r = g * BLOCKS + first // P + q
                 nc.scalar.activation(
-                    out=gate[:, q * P : (q + 1) * P],
+                    out=gate_t[:, q * P : (q + 1) * P],
                     in_=z[:, q * P : (q + 1) * P],
                     func=ACT.Sigmoid,
                     bias=bias_cols[:, r : r + 1],
                 )
+            gate = psum_out.tile([P, PIECE], F32)
+            for q in range(PIECE_BLOCKS):
+                block = slice(q * P, (q + 1) * P)
+                nc.tensor.transpose(gate[:, block], gate_t[:, block], ident_f32[:])
             if g == 0:
                 nc.vector.tensor_mul(out=i_cand[:, cols], in0=gate[:], in1=cand[:, cols])
             elif g == 1:
-                nc.vector.tensor_mul(out=f_c[:, cols], in0=gate[:], in1=cell_t[:, 1, cols])
+                nc.vector.tensor_mul(out=f_c[:, cols], in0=gate[:], in1=cell_in[:, 1, cols])
                 nc.vector.tensor_add(out=c_new[:, cols], in0=f_c[:, cols], in1=i_cand[:, cols])
                 nc.scalar.activation(out=tanh_c[:, cols], in_=c_new[:, cols], func=ACT.Tanh)
-                store_piece(out_1, c_new, first, nc.vector.tensor_copy)
+                nc.sync.dma_start(out=out_1[:, cols], in_=c_new[:, cols])
             else:
                 nc.vector.tensor_mul(out=h_new[:, cols], in0=gate[:], in1=tanh_c[:, cols])
-                store_piece(out_0, h_new, first, nc.scalar.copy)
+                nc.sync.dma_start(out=out_0[:, cols], in_=h_new[:, cols])
 
         grouped_next = regroup(raws[0])
         for m, (g, first) in enumerate(pieces):

@@ -85,7 +85,7 @@ def tile_rlstmcell_pb_s_kernel(
             for u in range(2):
                 nc.tensor.transpose(xh_t[:, a, u, :], xh_words[:, a, u, :], ident_f32[:])
         xh_grouped = consts.tile([P, OPERANDS * P * PACK], BF16, align_bytes=64)
-        nc.vector.tensor_copy(
+        nc.scalar.copy(
             out=xh_grouped[:].bitcast(F32).rearrange("p (a b u) -> p a b u", a=OPERANDS, u=2),
             in_=xh_t[:].rearrange("p a u b -> p a b u"),
         )
@@ -116,10 +116,24 @@ def tile_rlstmcell_pb_s_kernel(
         i_cand = consts.tile([P, D], F32)
         f_c = consts.tile([P, D], F32)
 
-        def finish_piece(g, first, z):
-            cols = slice(first, first + PIECE)
-            gate_t = wpool.tile([P, PIECE], F32)
-            for q in range(PIECE_BLOCKS):
+        def finish_columns(g, first, width, codes, scales, at):
+            cols = slice(first, first + width)
+            z = psum_gate.tile([P, width], F32)
+            for q in range(width // P):
+                block = slice(q * P, (q + 1) * P)
+                w_block = slice(at + q * P, at + (q + 1) * P)
+                for a in range(OPERANDS):
+                    nc.tensor.matmul_mx(
+                        out=z[:, block],
+                        lhsT=codes[:, a, w_block].bitcast(FP8X4),
+                        lhsT_scale=scales[:, a, w_block],
+                        rhs=xh_codes[:, a * P : (a + 1) * P].bitcast(FP8X4),
+                        rhs_scale=xh_scales[:, a * P : (a + 1) * P],
+                        start=(a == 0),
+                        stop=(a == OPERANDS - 1),
+                    )
+            gate_t = wpool.tile([P, width], F32)
+            for q in range(width // P):
                 r = g * BLOCKS + first // P + q
                 nc.scalar.activation(
                     out=gate_t[:, q * P : (q + 1) * P],
@@ -127,8 +141,8 @@ def tile_rlstmcell_pb_s_kernel(
                     func=ACT.Sigmoid,
                     bias=bias_cols[:, r : r + 1],
                 )
-            gate = psum_out.tile([P, PIECE], F32)
-            for q in range(PIECE_BLOCKS):
+            gate = psum_out.tile([P, width], F32)
+            for q in range(width // P):
                 block = slice(q * P, (q + 1) * P)
                 nc.tensor.transpose(gate[:, block], gate_t[:, block], ident_f32[:])
             if g == 0:
@@ -154,17 +168,6 @@ def tile_rlstmcell_pb_s_kernel(
                 scales=scales[:].rearrange("p a n -> p (a n)"),
                 in_=grouped[:].rearrange("p a n j -> p (a n j)"),
             )
-            z = psum_gate.tile([P, PIECE], F32)
-            for q in range(PIECE_BLOCKS):
-                block = slice(q * P, (q + 1) * P)
-                for a in range(OPERANDS):
-                    nc.tensor.matmul_mx(
-                        out=z[:, block],
-                        lhsT=codes[:, a, block].bitcast(FP8X4),
-                        lhsT_scale=scales[:, a, block],
-                        rhs=xh_codes[:, a * P : (a + 1) * P].bitcast(FP8X4),
-                        rhs_scale=xh_scales[:, a * P : (a + 1) * P],
-                        start=(a == 0),
-                        stop=(a == OPERANDS - 1),
-                    )
-            finish_piece(g, first, z)
+            width = P if m == len(pieces) - 1 else PIECE
+            for at in range(0, PIECE, width):
+                finish_columns(g, first + at, width, codes, scales, at)

@@ -9,6 +9,7 @@ U32 = mybir.dt.uint32
 U8 = mybir.dt.uint8
 FP8X4 = mybir.dt.float8_e4m3fn_x4
 ACT = mybir.ActivationFunctionType
+ENGINE = mybir.EngineType
 
 P = 128
 PACK = 4
@@ -72,102 +73,140 @@ def tile_rlstmcell_pb_s_kernel(
         nc.vector.memset(warm[:], 0.0)
         nc.scalar.activation(out=warm[:], in_=warm[:], func=ACT.Sigmoid)
 
-        bias_cols_ps = psum_in.tile([P, P], BF16)
-        nc.tensor.transpose(bias_cols_ps[:], bias_rows[:], ident_bf[:])
         bias_cols = consts.tile([P, GATES * BLOCKS], F32)
-        nc.vector.tensor_copy(out=bias_cols[:], in_=bias_cols_ps[:, 0 : GATES * BLOCKS])
-
-        xh_words = xh[:].rearrange("b a k -> b (a k)").bitcast(F32).rearrange(
-            "b (a p u) -> b a u p", a=OPERANDS, u=2
-        )
-        xh_t = psum_in.tile([P, OPERANDS, 2, P], F32)
-        for a in range(OPERANDS):
-            for u in range(2):
-                nc.tensor.transpose(xh_t[:, a, u, :], xh_words[:, a, u, :], ident_f32[:])
         xh_grouped = consts.tile([P, OPERANDS * P * PACK], BF16, align_bytes=64)
-        nc.scalar.copy(
-            out=xh_grouped[:].bitcast(F32).rearrange("p (a b u) -> p a b u", a=OPERANDS, u=2),
-            in_=xh_t[:].rearrange("p a u b -> p a b u"),
-        )
         xh_codes = consts.tile([P, OPERANDS * P], U32, align_bytes=64)
         xh_scales = consts.tile([P, OPERANDS * P], U8, align_bytes=64)
-        nc.vector.quantize_mx(
-            out=xh_codes[:].bitcast(FP8X4), scales=xh_scales[:], in_=xh_grouped[:]
-        )
-
         cand = consts.tile([P, D], F32)
-        nc.scalar.activation(out=cand[:], in_=cell_in[:, 0, :], func=ACT.Tanh)
-
-        def regroup(raw):
-            grouped = wpool.tile([P, OPERANDS, PIECE, PACK], BF16, align_bytes=64)
-            nc.vector.tensor_copy(
-                out=grouped[:, 0, :, :].rearrange("p (c i) j -> p c j i", i=4),
-                in_=raw[:, 0, :, :].rearrange("p j (c i) -> p c j i", i=4),
-            )
-            nc.scalar.copy(
-                out=grouped[:, 1, :, :].rearrange("p (c i) j -> p c j i", i=4),
-                in_=raw[:, 1, :, :].rearrange("p j (c i) -> p c j i", i=4),
-            )
-            return grouped
-
         c_new = consts.tile([P, D], F32)
         tanh_c = consts.tile([P, D], F32)
         h_new = consts.tile([P, D], F32)
         i_cand = consts.tile([P, D], F32)
         f_c = consts.tile([P, D], F32)
 
-        def finish_columns(g, first, width, codes, scales, at):
-            cols = slice(first, first + width)
-            z = psum_gate.tile([P, width], F32)
-            for q in range(width // P):
-                block = slice(q * P, (q + 1) * P)
-                w_block = slice(at + q * P, at + (q + 1) * P)
-                for a in range(OPERANDS):
-                    nc.tensor.matmul_mx(
-                        out=z[:, block],
-                        lhsT=codes[:, a, w_block].bitcast(FP8X4),
-                        lhsT_scale=scales[:, a, w_block],
-                        rhs=xh_codes[:, a * P : (a + 1) * P].bitcast(FP8X4),
-                        rhs_scale=xh_scales[:, a * P : (a + 1) * P],
-                        start=(a == 0),
-                        stop=(a == OPERANDS - 1),
-                    )
-            gate_t = wpool.tile([P, width], F32)
-            for q in range(width // P):
-                r = g * BLOCKS + first // P + q
-                nc.scalar.activation(
-                    out=gate_t[:, q * P : (q + 1) * P],
-                    in_=z[:, q * P : (q + 1) * P],
-                    func=ACT.Sigmoid,
-                    bias=bias_cols[:, r : r + 1],
-                )
-            gate = psum_out.tile([P, width], F32)
-            for q in range(width // P):
-                block = slice(q * P, (q + 1) * P)
-                nc.tensor.transpose(gate[:, block], gate_t[:, block], ident_f32[:])
-            if g == 0:
-                nc.vector.tensor_mul(out=i_cand[:, cols], in0=gate[:], in1=cand[:, cols])
-            elif g == 1:
-                nc.vector.tensor_mul(out=f_c[:, cols], in0=gate[:], in1=cell_in[:, 1, cols])
-                nc.vector.tensor_add(out=c_new[:, cols], in0=f_c[:, cols], in1=i_cand[:, cols])
-                nc.scalar.activation(out=tanh_c[:, cols], in_=c_new[:, cols], func=ACT.Tanh)
-                nc.sync.dma_start(out=out_1[:, cols], in_=c_new[:, cols])
-            else:
-                nc.vector.tensor_mul(out=h_new[:, cols], in0=gate[:], in1=tanh_c[:, cols])
-                nc.sync.dma_start(out=out_0[:, cols], in_=h_new[:, cols])
+        def prepare_small_inputs():
+            bias_cols_ps = psum_in.tile([P, P], BF16)
+            nc.tensor.transpose(bias_cols_ps[:], bias_rows[:], ident_bf[:])
+            nc.vector.tensor_copy(out=bias_cols[:], in_=bias_cols_ps[:, 0 : GATES * BLOCKS])
+            nc.scalar.activation(out=cand[:], in_=cell_in[:, 0, :], func=ACT.Tanh)
+            xh_words = xh[:].rearrange("b a k -> b (a k)").bitcast(F32).rearrange(
+                "b (a p u) -> b a u p", a=OPERANDS, u=2
+            )
+            xh_t = psum_in.tile([P, OPERANDS, 2, P], F32)
+            for a in range(OPERANDS):
+                for u in range(2):
+                    nc.tensor.transpose(xh_t[:, a, u, :], xh_words[:, a, u, :], ident_f32[:])
+            nc.scalar.copy(
+                out=xh_grouped[:].bitcast(F32).rearrange("p (a b u) -> p a b u", a=OPERANDS, u=2),
+                in_=xh_t[:].rearrange("p a u b -> p a b u"),
+            )
 
-        grouped_next = regroup(raws[0])
-        for m, (g, first) in enumerate(pieces):
-            grouped = grouped_next
-            if m + 1 < len(pieces):
-                grouped_next = regroup(raws[m + 1])
+        def quantise_small_inputs():
+            nc.vector.quantize_mx(
+                out=xh_codes[:].bitcast(FP8X4), scales=xh_scales[:], in_=xh_grouped[:]
+            )
+
+        groupeds, codes_of, scales_of, sums_of, gates_of = {}, {}, {}, {}, {}
+
+        def units(m):
+            width = P if m == len(pieces) - 1 else PIECE
+            return [(at, width) for at in range(0, PIECE, width)]
+
+        def regroup(m):
+            raw = raws[m]
+            grouped = wpool.tile([P, OPERANDS, PIECE, PACK], BF16, align_bytes=64)
+            nc.scalar.copy(
+                out=grouped[:, 1, :, :].rearrange("p (c i) j -> p c j i", i=4),
+                in_=raw[:, 1, :, :].rearrange("p j (c i) -> p c j i", i=4),
+            )
+            nc.vector.tensor_copy(
+                out=grouped[:, 0, :, :].rearrange("p (c i) j -> p c j i", i=4),
+                in_=raw[:, 0, :, :].rearrange("p j (c i) -> p c j i", i=4),
+            )
+            groupeds[m] = grouped
+
+        def quantise(m):
             codes = wpool.tile([P, OPERANDS, PIECE], U32, align_bytes=64)
             scales = wpool.tile([P, OPERANDS, PIECE], U8, align_bytes=64)
             nc.vector.quantize_mx(
                 out=codes[:].rearrange("p a n -> p (a n)").bitcast(FP8X4),
                 scales=scales[:].rearrange("p a n -> p (a n)"),
-                in_=grouped[:].rearrange("p a n j -> p (a n j)"),
+                in_=groupeds[m][:].rearrange("p a n j -> p (a n j)"),
             )
-            width = P if m == len(pieces) - 1 else PIECE
-            for at in range(0, PIECE, width):
-                finish_columns(g, first + at, width, codes, scales, at)
+            codes_of[m], scales_of[m] = codes, scales
+
+        def multiply(m):
+            sums_of[m] = []
+            for at, width in units(m):
+                z = psum_gate.tile([P, width], F32)
+                for q in range(width // P):
+                    w_block = slice(at + q * P, at + (q + 1) * P)
+                    for a in range(OPERANDS):
+                        nc.tensor.matmul_mx(
+                            out=z[:, q * P : (q + 1) * P],
+                            lhsT=codes_of[m][:, a, w_block].bitcast(FP8X4),
+                            lhsT_scale=scales_of[m][:, a, w_block],
+                            rhs=xh_codes[:, a * P : (a + 1) * P].bitcast(FP8X4),
+                            rhs_scale=xh_scales[:, a * P : (a + 1) * P],
+                            start=(a == 0),
+                            stop=(a == OPERANDS - 1),
+                        )
+                sums_of[m].append(z)
+
+        def squash(m):
+            g, first = pieces[m]
+            gates_of[m] = []
+            for (at, width), z in zip(units(m), sums_of[m]):
+                gate_t = wpool.tile([P, width], F32)
+                gate = psum_out.tile([P, width], F32)
+                for q in range(width // P):
+                    block = slice(q * P, (q + 1) * P)
+                    r = g * BLOCKS + (first + at) // P + q
+                    nc.scalar.activation(
+                        out=gate_t[:, block], in_=z[:, block], func=ACT.Sigmoid, bias=bias_cols[:, r : r + 1]
+                    )
+                for q in range(width // P):
+                    block = slice(q * P, (q + 1) * P)
+                    nc.tensor.transpose(gate[:, block], gate_t[:, block], ident_f32[:])
+                gates_of[m].append(gate)
+
+        def products(m):
+            g, first = pieces[m]
+            for (at, width), gate in zip(units(m), gates_of[m]):
+                cols = slice(first + at, first + at + width)
+                if g == 0:
+                    nc.vector.tensor_mul(out=i_cand[:, cols], in0=gate[:], in1=cand[:, cols])
+                elif g == 1:
+                    nc.vector.tensor_mul(out=f_c[:, cols], in0=gate[:], in1=cell_in[:, 1, cols])
+                    nc.vector.tensor_add(out=c_new[:, cols], in0=f_c[:, cols], in1=i_cand[:, cols])
+                    nc.sync.dma_start(out=out_1[:, cols], in_=c_new[:, cols])
+                else:
+                    nc.vector.tensor_mul(out=h_new[:, cols], in0=gate[:], in1=tanh_c[:, cols])
+                    nc.sync.dma_start(out=out_0[:, cols], in_=h_new[:, cols])
+
+        def tanh_of_cell(m):
+            g, first = pieces[m]
+            if g == 1:
+                cols = slice(first, first + PIECE)
+                nc.scalar.activation(out=tanh_c[:, cols], in_=c_new[:, cols], func=ACT.Tanh)
+
+        n = len(pieces)
+        with tc.manual_schedule(engines={ENGINE.DVE, ENGINE.Activation, ENGINE.PE}):
+            for t in range(n + 4):
+                if t < n:
+                    regroup(t)
+                if 0 <= t - 4 < n:
+                    products(t - 4)
+                if 0 <= t - 1 < n:
+                    quantise(t - 1)
+                if t == 1:
+                    prepare_small_inputs()
+                if t == 2:
+                    quantise_small_inputs()
+                    multiply(0)
+                if 1 <= t - 1 < n:
+                    multiply(t - 1)
+                if 0 <= t - 2 < n:
+                    squash(t - 2)
+                if 0 <= t - 4 < n:
+                    tanh_of_cell(t - 4)

@@ -108,44 +108,52 @@ def tile_rlstmcell_pb_s_kernel(
 
         groupeds, codes_of, scales_of, sums_of, gates_of = {}, {}, {}, {}, {}
 
+        def parts(m):
+            return 2 if m == len(pieces) - 1 else 1
+
         def units(m):
-            width = P if m == len(pieces) - 1 else PIECE
+            width = PIECE // parts(m)
             return [(at, width) for at in range(0, PIECE, width)]
 
+        def regroup_columns(copy, m, a, part):
+            at, width = units(m)[part]
+            copy(
+                out=groupeds[m][:, part, a, :, :].rearrange("p (c i) j -> p c j i", i=4),
+                in_=raws[m][:, a, :, at : at + width].rearrange("p j (c i) -> p c j i", i=4),
+            )
+
         def regroup(m):
-            raw = raws[m]
-            grouped = wpool.tile([P, OPERANDS, PIECE, PACK], BF16, align_bytes=64)
-            nc.scalar.copy(
-                out=grouped[:, 1, :, :].rearrange("p (c i) j -> p c j i", i=4),
-                in_=raw[:, 1, :, :].rearrange("p j (c i) -> p c j i", i=4),
-            )
-            nc.vector.tensor_copy(
-                out=grouped[:, 0, :, :].rearrange("p (c i) j -> p c j i", i=4),
-                in_=raw[:, 0, :, :].rearrange("p j (c i) -> p c j i", i=4),
-            )
+            grouped = wpool.tile([P, parts(m), OPERANDS, PIECE // parts(m), PACK], BF16, align_bytes=64)
             groupeds[m] = grouped
+            regroup_columns(nc.scalar.copy, m, 1, 0)
+            for part in range(parts(m)):
+                regroup_columns(nc.vector.tensor_copy, m, 0, part)
+
+        def regroup_last_part():
+            regroup_columns(nc.vector.tensor_copy, len(pieces) - 1, 1, 1)
 
         def quantise(m):
-            codes = wpool.tile([P, OPERANDS, PIECE], U32, align_bytes=64)
-            scales = wpool.tile([P, OPERANDS, PIECE], U8, align_bytes=64)
-            nc.vector.quantize_mx(
-                out=codes[:].rearrange("p a n -> p (a n)").bitcast(FP8X4),
-                scales=scales[:].rearrange("p a n -> p (a n)"),
-                in_=groupeds[m][:].rearrange("p a n j -> p (a n j)"),
-            )
+            codes = wpool.tile([P, parts(m), OPERANDS, PIECE // parts(m)], U32, align_bytes=64)
+            scales = wpool.tile([P, parts(m), OPERANDS, PIECE // parts(m)], U8, align_bytes=64)
+            for part in range(parts(m)):
+                nc.vector.quantize_mx(
+                    out=codes[:, part, :, :].rearrange("p a n -> p (a n)").bitcast(FP8X4),
+                    scales=scales[:, part, :, :].rearrange("p a n -> p (a n)"),
+                    in_=groupeds[m][:, part, :, :, :].rearrange("p a n j -> p (a n j)"),
+                )
             codes_of[m], scales_of[m] = codes, scales
 
         def multiply(m):
             sums_of[m] = []
-            for at, width in units(m):
+            for part, (at, width) in enumerate(units(m)):
                 z = psum_gate.tile([P, width], F32)
                 for q in range(width // P):
-                    w_block = slice(at + q * P, at + (q + 1) * P)
+                    block = slice(q * P, (q + 1) * P)
                     for a in range(OPERANDS):
                         nc.tensor.matmul_mx(
-                            out=z[:, q * P : (q + 1) * P],
-                            lhsT=codes_of[m][:, a, w_block].bitcast(FP8X4),
-                            lhsT_scale=scales_of[m][:, a, w_block],
+                            out=z[:, block],
+                            lhsT=codes_of[m][:, part, a, block].bitcast(FP8X4),
+                            lhsT_scale=scales_of[m][:, part, a, block],
                             rhs=xh_codes[:, a * P : (a + 1) * P].bitcast(FP8X4),
                             rhs_scale=xh_scales[:, a * P : (a + 1) * P],
                             start=(a == 0),
@@ -204,6 +212,8 @@ def tile_rlstmcell_pb_s_kernel(
                 if t == 2:
                     quantise_small_inputs()
                     multiply(0)
+                if t == n - 1:
+                    regroup_last_part()
                 if 1 <= t - 1 < n:
                     multiply(t - 1)
                 if 0 <= t - 2 < n:

@@ -17,9 +17,8 @@ D = 512
 GATES = 3
 OPERANDS = 2
 BLOCKS = D // P
-PIECE = 256
-PIECES = D // PIECE
-PIECE_BLOCKS = PIECE // P
+HALF = 256
+HALVES = D // HALF
 
 FLOPS = 2 * P * D * (GATES * D) * OPERANDS
 
@@ -29,41 +28,42 @@ def tile_rlstmcell_pb_s_kernel(
 ):
     nc = tc.nc
     weights = (kernel, recurrent_kernel)
-    pieces = [(g, s * PIECE) for g in range(GATES) for s in range(PIECES)]
 
     with ExitStack() as ctx:
         consts = ctx.enter_context(tc.tile_pool(name="consts", bufs=1))
-        wpool = ctx.enter_context(tc.tile_pool(name="wpool", bufs=len(pieces)))
+        wpool = ctx.enter_context(tc.tile_pool(name="wpool", bufs=GATES * HALVES + 1))
         psum_in = ctx.enter_context(tc.psum_pool(name="psum_in", bufs=1))
         psum_gate = ctx.enter_context(tc.psum_pool(name="psum_gate", bufs=3))
         psum_out = ctx.enter_context(tc.psum_pool(name="psum_out", bufs=3))
 
-        def load_piece(g, first):
-            raw = wpool.tile([P, OPERANDS, PACK, PIECE], BF16)
-            for a in range(OPERANDS):
-                nc.sync.dma_start(
-                    out=raw[:, a, :, :],
-                    in_=weights[a][:, g * D + first : g * D + first + PIECE].rearrange(
-                        "(p j) n -> p j n", j=PACK
-                    ),
-                )
-            return raw
-
-        raws = [load_piece(*pieces[0]), load_piece(*pieces[1])]
         bias_rows = consts.tile([P, P], BF16)
         nc.vector.memset(bias_rows[:], 0.0)
-        nc.sync.dma_start(
+        nc.gpsimd.dma_start(
             out=bias_rows[0 : GATES * BLOCKS, :], in_=bias.rearrange("(r c) -> r c", c=P)
         )
+
+        raws = {}
+
+        def load_weight(g, a):
+            raw = wpool.tile([P, PACK, D], BF16)
+            nc.sync.dma_start(
+                out=raw[:],
+                in_=weights[a][:, g * D : (g + 1) * D].rearrange("(p j) n -> p j n", j=PACK),
+            )
+            raws[g, a] = raw
+
+        load_weight(0, 0)
         xh = consts.tile([P, OPERANDS, D], BF16)
         nc.sync.dma_start(out=xh[:, 0, :], in_=inputs)
         nc.sync.dma_start(out=xh[:, 1, :], in_=h_state)
+        load_weight(0, 1)
         cell_in = consts.tile([P, 2, D], BF16)
         nc.sync.dma_start(out=cell_in[:, 0, :], in_=c_upd.rearrange("b s d -> b (s d)"))
-        raws.append(load_piece(*pieces[2]))
+        load_weight(1, 0)
+        load_weight(1, 1)
         nc.sync.dma_start(out=cell_in[:, 1, :], in_=c_state)
-        for piece in pieces[3:]:
-            raws.append(load_piece(*piece))
+        load_weight(2, 0)
+        load_weight(2, 1)
 
         ident_f32 = consts.tile([P, P], F32)
         make_identity(nc, ident_f32[:])
@@ -84,11 +84,7 @@ def tile_rlstmcell_pb_s_kernel(
         i_cand = consts.tile([P, D], F32)
         f_c = consts.tile([P, D], F32)
 
-        def prepare_small_inputs():
-            bias_cols_ps = psum_in.tile([P, P], BF16)
-            nc.tensor.transpose(bias_cols_ps[:], bias_rows[:], ident_bf[:])
-            nc.vector.tensor_copy(out=bias_cols[:], in_=bias_cols_ps[:, 0 : GATES * BLOCKS])
-            nc.scalar.activation(out=cand[:], in_=cell_in[:, 0, :], func=ACT.Tanh)
+        def transpose_inputs():
             xh_words = xh[:].rearrange("b a k -> b (a k)").bitcast(F32).rearrange(
                 "b (a p u) -> b a u p", a=OPERANDS, u=2
             )
@@ -101,122 +97,156 @@ def tile_rlstmcell_pb_s_kernel(
                 in_=xh_t[:].rearrange("p a u b -> p a b u"),
             )
 
-        def quantise_small_inputs():
+        def transpose_bias():
+            bias_cols_ps = psum_in.tile([P, P], BF16)
+            nc.tensor.transpose(bias_cols_ps[:], bias_rows[:], ident_bf[:])
+            nc.vector.tensor_copy(out=bias_cols[:], in_=bias_cols_ps[:, 0 : GATES * BLOCKS])
+
+        def candidate():
+            nc.scalar.activation(out=cand[:], in_=cell_in[:, 0, :], func=ACT.Tanh)
+
+        def quantise_inputs():
             nc.vector.quantize_mx(
                 out=xh_codes[:].bitcast(FP8X4), scales=xh_scales[:], in_=xh_grouped[:]
             )
 
+        pieces = {(g, s): (s * HALF, HALF) for g in range(GATES) for s in range(HALVES)}
+        pieces[2, 1] = (HALF, P)
+        pieces[2, 2] = (HALF + P, P)
         groupeds, codes_of, scales_of, sums_of, gates_of = {}, {}, {}, {}, {}
+        for piece, (first, width) in pieces.items():
+            grouped = wpool.tile([P, OPERANDS, width, PACK], BF16, align_bytes=64)
+            groupeds[piece] = grouped
 
-        def parts(m):
-            return 2 if m == len(pieces) - 1 else 1
-
-        def units(m):
-            width = PIECE // parts(m)
-            return [(at, width) for at in range(0, PIECE, width)]
-
-        def regroup_columns(copy, m, a, part):
-            at, width = units(m)[part]
+        def regroup(copy, piece, a):
+            first, width = pieces[piece]
             copy(
-                out=groupeds[m][:, part, a, :, :].rearrange("p (c i) j -> p c j i", i=4),
-                in_=raws[m][:, a, :, at : at + width].rearrange("p j (c i) -> p c j i", i=4),
+                out=groupeds[piece][:, a, :, :].rearrange("p (c i) j -> p c j i", i=4),
+                in_=raws[piece[0], a][:, :, first : first + width].rearrange("p j (c i) -> p c j i", i=4),
             )
 
-        def regroup(m):
-            grouped = wpool.tile([P, parts(m), OPERANDS, PIECE // parts(m), PACK], BF16, align_bytes=64)
-            groupeds[m] = grouped
-            regroup_columns(nc.scalar.copy, m, 1, 0)
-            for part in range(parts(m)):
-                regroup_columns(nc.vector.tensor_copy, m, 0, part)
+        def quantise(piece):
+            first, width = pieces[piece]
+            codes = wpool.tile([P, OPERANDS, width], U32, align_bytes=64)
+            scales = wpool.tile([P, OPERANDS, width], U8, align_bytes=64)
+            nc.vector.quantize_mx(
+                out=codes[:].rearrange("p a n -> p (a n)").bitcast(FP8X4),
+                scales=scales[:].rearrange("p a n -> p (a n)"),
+                in_=groupeds[piece][:].rearrange("p a n j -> p (a n j)"),
+            )
+            codes_of[piece], scales_of[piece] = codes, scales
 
-        def regroup_last_part():
-            regroup_columns(nc.vector.tensor_copy, len(pieces) - 1, 1, 1)
-
-        def quantise(m):
-            codes = wpool.tile([P, parts(m), OPERANDS, PIECE // parts(m)], U32, align_bytes=64)
-            scales = wpool.tile([P, parts(m), OPERANDS, PIECE // parts(m)], U8, align_bytes=64)
-            for part in range(parts(m)):
-                nc.vector.quantize_mx(
-                    out=codes[:, part, :, :].rearrange("p a n -> p (a n)").bitcast(FP8X4),
-                    scales=scales[:, part, :, :].rearrange("p a n -> p (a n)"),
-                    in_=groupeds[m][:, part, :, :, :].rearrange("p a n j -> p (a n j)"),
-                )
-            codes_of[m], scales_of[m] = codes, scales
-
-        def multiply(m):
-            sums_of[m] = []
-            for part, (at, width) in enumerate(units(m)):
-                z = psum_gate.tile([P, width], F32)
-                for q in range(width // P):
-                    block = slice(q * P, (q + 1) * P)
-                    for a in range(OPERANDS):
-                        nc.tensor.matmul_mx(
-                            out=z[:, block],
-                            lhsT=codes_of[m][:, part, a, block].bitcast(FP8X4),
-                            lhsT_scale=scales_of[m][:, part, a, block],
-                            rhs=xh_codes[:, a * P : (a + 1) * P].bitcast(FP8X4),
-                            rhs_scale=xh_scales[:, a * P : (a + 1) * P],
-                            start=(a == 0),
-                            stop=(a == OPERANDS - 1),
-                        )
-                sums_of[m].append(z)
-
-        def squash(m):
-            g, first = pieces[m]
-            gates_of[m] = []
-            for (at, width), z in zip(units(m), sums_of[m]):
-                gate_t = wpool.tile([P, width], F32)
-                gate = psum_out.tile([P, width], F32)
-                for q in range(width // P):
-                    block = slice(q * P, (q + 1) * P)
-                    r = g * BLOCKS + (first + at) // P + q
-                    nc.scalar.activation(
-                        out=gate_t[:, block], in_=z[:, block], func=ACT.Sigmoid, bias=bias_cols[:, r : r + 1]
+        def multiply(piece):
+            first, width = pieces[piece]
+            z = psum_gate.tile([P, width], F32)
+            for q in range(width // P):
+                block = slice(q * P, (q + 1) * P)
+                for a in range(OPERANDS):
+                    nc.tensor.matmul_mx(
+                        out=z[:, block],
+                        lhsT=codes_of[piece][:, a, block].bitcast(FP8X4),
+                        lhsT_scale=scales_of[piece][:, a, block],
+                        rhs=xh_codes[:, a * P : (a + 1) * P].bitcast(FP8X4),
+                        rhs_scale=xh_scales[:, a * P : (a + 1) * P],
+                        start=(a == 0),
+                        stop=(a == OPERANDS - 1),
                     )
-                for q in range(width // P):
-                    block = slice(q * P, (q + 1) * P)
-                    nc.tensor.transpose(gate[:, block], gate_t[:, block], ident_f32[:])
-                gates_of[m].append(gate)
+            sums_of[piece] = z
 
-        def products(m):
-            g, first = pieces[m]
-            for (at, width), gate in zip(units(m), gates_of[m]):
-                cols = slice(first + at, first + at + width)
-                if g == 0:
-                    nc.vector.tensor_mul(out=i_cand[:, cols], in0=gate[:], in1=cand[:, cols])
-                elif g == 1:
-                    nc.vector.tensor_mul(out=f_c[:, cols], in0=gate[:], in1=cell_in[:, 1, cols])
-                    nc.vector.tensor_add(out=c_new[:, cols], in0=f_c[:, cols], in1=i_cand[:, cols])
-                    nc.sync.dma_start(out=out_1[:, cols], in_=c_new[:, cols])
-                else:
-                    nc.vector.tensor_mul(out=h_new[:, cols], in0=gate[:], in1=tanh_c[:, cols])
-                    nc.sync.dma_start(out=out_0[:, cols], in_=h_new[:, cols])
+        def squash(piece):
+            first, width = pieces[piece]
+            gate_t = wpool.tile([P, width], F32)
+            gate = psum_out.tile([P, width], F32)
+            for q in range(width // P):
+                block = slice(q * P, (q + 1) * P)
+                r = piece[0] * BLOCKS + first // P + q
+                nc.scalar.activation(
+                    out=gate_t[:, block],
+                    in_=sums_of[piece][:, block],
+                    func=ACT.Sigmoid,
+                    bias=bias_cols[:, r : r + 1],
+                )
+            for q in range(width // P):
+                block = slice(q * P, (q + 1) * P)
+                nc.tensor.transpose(gate[:, block], gate_t[:, block], ident_f32[:])
+            gates_of[piece] = gate
 
-        def tanh_of_cell(m):
-            g, first = pieces[m]
-            if g == 1:
-                cols = slice(first, first + PIECE)
-                nc.scalar.activation(out=tanh_c[:, cols], in_=c_new[:, cols], func=ACT.Tanh)
+        def columns(piece):
+            first, width = pieces[piece]
+            return slice(first, first + width)
 
-        n = len(pieces)
+        def times_candidate(s):
+            cols = columns((0, s))
+            nc.vector.tensor_mul(out=i_cand[:, cols], in0=gates_of[0, s][:], in1=cand[:, cols])
+
+        def times_cell(s):
+            cols = columns((1, s))
+            nc.vector.tensor_mul(out=f_c[:, cols], in0=gates_of[1, s][:], in1=cell_in[:, 1, cols])
+
+        def new_cell(s):
+            cols = columns((1, s))
+            nc.vector.tensor_add(out=c_new[:, cols], in0=f_c[:, cols], in1=i_cand[:, cols])
+            nc.sync.dma_start(out=out_1[:, cols], in_=c_new[:, cols])
+
+        def tanh_of_cell(s):
+            cols = columns((1, s))
+            nc.scalar.activation(out=tanh_c[:, cols], in_=c_new[:, cols], func=ACT.Tanh)
+
+        def new_hidden(s):
+            cols = columns((2, s))
+            nc.vector.tensor_mul(out=h_new[:, cols], in0=gates_of[2, s][:], in1=tanh_c[:, cols])
+            nc.sync.dma_start(out=out_0[:, cols], in_=h_new[:, cols])
+
+        by_vector, by_scalar = nc.vector.tensor_copy, nc.scalar.copy
+
         with tc.manual_schedule(engines={ENGINE.DVE, ENGINE.Activation, ENGINE.PE}):
-            for t in range(n + 4):
-                if t < n:
-                    regroup(t)
-                if 0 <= t - 4 < n:
-                    products(t - 4)
-                if 0 <= t - 1 < n:
-                    quantise(t - 1)
-                if t == 1:
-                    prepare_small_inputs()
-                if t == 2:
-                    quantise_small_inputs()
-                    multiply(0)
-                if t == n - 1:
-                    regroup_last_part()
-                if 1 <= t - 1 < n:
-                    multiply(t - 1)
-                if 0 <= t - 2 < n:
-                    squash(t - 2)
-                if 0 <= t - 4 < n:
-                    tanh_of_cell(t - 4)
+            regroup(by_vector, (0, 0), 0)
+            regroup(by_scalar, (0, 1), 0)
+            transpose_inputs()
+            regroup(by_vector, (0, 0), 1)
+            regroup(by_scalar, (0, 1), 1)
+            transpose_bias()
+            candidate()
+            quantise_inputs()
+            quantise((0, 0))
+            multiply((0, 0))
+            quantise((0, 1))
+            multiply((0, 1))
+            regroup(by_vector, (1, 0), 0)
+            regroup(by_scalar, (1, 1), 0)
+            squash((0, 0))
+            regroup(by_vector, (1, 0), 1)
+            regroup(by_scalar, (1, 1), 1)
+            quantise((1, 0))
+            multiply((1, 0))
+            squash((0, 1))
+            quantise((1, 1))
+            multiply((1, 1))
+            regroup(by_vector, (2, 0), 0)
+            regroup(by_scalar, (2, 1), 0)
+            regroup(by_scalar, (2, 2), 0)
+            times_candidate(0)
+            squash((1, 0))
+            regroup(by_vector, (2, 0), 1)
+            regroup(by_scalar, (2, 1), 1)
+            regroup(by_vector, (2, 2), 1)
+            squash((1, 1))
+            times_candidate(1)
+            quantise((2, 0))
+            multiply((2, 0))
+            times_cell(0)
+            quantise((2, 1))
+            multiply((2, 1))
+            times_cell(1)
+            quantise((2, 2))
+            multiply((2, 2))
+            new_cell(0)
+            new_cell(1)
+            squash((2, 0))
+            tanh_of_cell(0)
+            squash((2, 1))
+            squash((2, 2))
+            tanh_of_cell(1)
+            new_hidden(0)
+            new_hidden(1)
+            new_hidden(2)

@@ -36,12 +36,6 @@ def tile_rlstmcell_pb_s_kernel(
         psum_gate = ctx.enter_context(tc.psum_pool(name="psum_gate", bufs=3))
         psum_out = ctx.enter_context(tc.psum_pool(name="psum_out", bufs=3))
 
-        bias_rows = consts.tile([P, P], BF16)
-        nc.vector.memset(bias_rows[:], 0.0)
-        nc.gpsimd.dma_start(
-            out=bias_rows[0 : GATES * BLOCKS, :], in_=bias.rearrange("(r c) -> r c", c=P)
-        )
-
         raws = {}
 
         def load_weight(g, a):
@@ -56,6 +50,11 @@ def tile_rlstmcell_pb_s_kernel(
         xh = consts.tile([P, OPERANDS, D], BF16)
         nc.sync.dma_start(out=xh[:, 0, :], in_=inputs)
         nc.sync.dma_start(out=xh[:, 1, :], in_=h_state)
+        bias_rows = consts.tile([P, P], BF16)
+        nc.vector.memset(bias_rows[:], 0.0)
+        nc.sync.dma_start(
+            out=bias_rows[0 : GATES * BLOCKS, :], in_=bias.rearrange("(r c) -> r c", c=P)
+        )
         load_weight(0, 1)
         cell_in = consts.tile([P, 2, D], BF16)
         nc.sync.dma_start(out=cell_in[:, 0, :], in_=c_upd.rearrange("b s d -> b (s d)"))

@@ -38,13 +38,16 @@ def tile_rlstmcell_pb_s_kernel(
 
         raws = {}
 
-        def load_weight(g, a):
-            raw = wpool.tile([P, PACK, D], BF16)
+        def load_weight(g, a, first=0, width=D):
+            raw = wpool.tile([P, PACK, width], BF16)
+            at = g * D + first
             nc.sync.dma_start(
                 out=raw[:],
-                in_=weights[a][:, g * D : (g + 1) * D].rearrange("(p j) n -> p j n", j=PACK),
+                in_=weights[a][:, at : at + width].rearrange("(p j) n -> p j n", j=PACK),
             )
-            raws[g, a] = raw
+            raws[g, a, first] = raw
+            if width == D:
+                raws[g, a, HALF] = raw[:, :, HALF:D]
 
         load_weight(0, 0)
         xh = consts.tile([P, OPERANDS, D], BF16)
@@ -62,7 +65,8 @@ def tile_rlstmcell_pb_s_kernel(
         load_weight(1, 1)
         nc.sync.dma_start(out=cell_in[:, 1, :], in_=c_state)
         load_weight(2, 0)
-        load_weight(2, 1)
+        load_weight(2, 1, 0, HALF)
+        load_weight(2, 1, HALF, HALF)
 
         ident_f32 = consts.tile([P, P], F32)
         make_identity(nc, ident_f32[:])
@@ -112,16 +116,20 @@ def tile_rlstmcell_pb_s_kernel(
         pieces = {(g, s): (s * HALF, HALF) for g in range(GATES) for s in range(HALVES)}
         pieces[2, 1] = (HALF, P)
         pieces[2, 2] = (HALF + P, P)
-        groupeds, codes_of, scales_of, sums_of, gates_of = {}, {}, {}, {}, {}
+        groupeds, codes_of, scales_of, sums_of, turned_of, gates_of = {}, {}, {}, {}, {}, {}
         for piece, (first, width) in pieces.items():
             grouped = wpool.tile([P, OPERANDS, width, PACK], BF16, align_bytes=64)
             groupeds[piece] = grouped
 
-        def regroup(copy, piece, a):
-            first, width = pieces[piece]
+        def regroup(copy, piece, a, at=0, width=None):
+            first, whole = pieces[piece]
+            width = width or whole
+            half = first // HALF * HALF
+            raw = raws[piece[0], a, half]
+            col = first - half + at
             copy(
-                out=groupeds[piece][:, a, :, :].rearrange("p (c i) j -> p c j i", i=4),
-                in_=raws[piece[0], a][:, :, first : first + width].rearrange("p j (c i) -> p c j i", i=4),
+                out=groupeds[piece][:, a, at : at + width, :].rearrange("p (c i) j -> p c j i", i=4),
+                in_=raw[:, :, col : col + width].rearrange("p j (c i) -> p c j i", i=4),
             )
 
         def quantise(piece):
@@ -155,7 +163,6 @@ def tile_rlstmcell_pb_s_kernel(
         def squash(piece):
             first, width = pieces[piece]
             gate_t = wpool.tile([P, width], F32)
-            gate = psum_out.tile([P, width], F32)
             for q in range(width // P):
                 block = slice(q * P, (q + 1) * P)
                 r = piece[0] * BLOCKS + first // P + q
@@ -165,6 +172,12 @@ def tile_rlstmcell_pb_s_kernel(
                     func=ACT.Sigmoid,
                     bias=bias_cols[:, r : r + 1],
                 )
+            turned_of[piece] = gate_t
+
+        def turn(piece):
+            first, width = pieces[piece]
+            gate_t = turned_of[piece]
+            gate = psum_out.tile([P, width], F32)
             for q in range(width // P):
                 block = slice(q * P, (q + 1) * P)
                 nc.tensor.transpose(gate[:, block], gate_t[:, block], ident_f32[:])
@@ -214,6 +227,7 @@ def tile_rlstmcell_pb_s_kernel(
             regroup(by_vector, (1, 0), 0)
             regroup(by_scalar, (1, 1), 0)
             squash((0, 0))
+            turn((0, 0))
             regroup(by_vector, (1, 0), 1)
             regroup(by_scalar, (1, 1), 1)
             quantise((1, 0))
@@ -221,31 +235,38 @@ def tile_rlstmcell_pb_s_kernel(
             squash((0, 1))
             quantise((1, 1))
             multiply((1, 1))
+            turn((0, 1))
             regroup(by_vector, (2, 0), 0)
             regroup(by_scalar, (2, 1), 0)
             regroup(by_scalar, (2, 2), 0)
             times_candidate(0)
+            regroup(by_vector, (2, 0), 1, 0, P)
+            regroup(by_scalar, (2, 0), 1, P, P)
             squash((1, 0))
-            regroup(by_vector, (2, 0), 1)
-            regroup(by_scalar, (2, 1), 1)
-            regroup(by_vector, (2, 2), 1)
+            turn((1, 0))
             squash((1, 1))
-            times_candidate(1)
+            turn((1, 1))
+            regroup(by_vector, (2, 1), 1)
+            regroup(by_scalar, (2, 2), 1)
             quantise((2, 0))
             multiply((2, 0))
-            times_cell(0)
             quantise((2, 1))
             multiply((2, 1))
-            times_cell(1)
+            times_candidate(1)
             quantise((2, 2))
             multiply((2, 2))
+            times_cell(0)
+            times_cell(1)
             new_cell(0)
             new_cell(1)
             squash((2, 0))
-            tanh_of_cell(0)
+            turn((2, 0))
             squash((2, 1))
             squash((2, 2))
+            tanh_of_cell(0)
             tanh_of_cell(1)
+            turn((2, 1))
+            turn((2, 2))
             new_hidden(0)
             new_hidden(1)
             new_hidden(2)

@@ -63,10 +63,10 @@ def tile_rlstmcell_pb_s_kernel(
         nc.sync.dma_start(out=cell_in[:, 0, :], in_=c_upd.rearrange("b s d -> b (s d)"))
         load_weight(1, 0)
         load_weight(1, 1)
-        nc.sync.dma_start(out=cell_in[:, 1, :], in_=c_state)
         load_weight(2, 0)
         load_weight(2, 1, 0, HALF)
         load_weight(2, 1, HALF, HALF)
+        nc.sync.dma_start(out=cell_in[:, 1, :], in_=c_state)
 
         ident_f32 = consts.tile([P, P], F32)
         make_identity(nc, ident_f32[:])

@@ -19,6 +19,7 @@ OPERANDS = 2
 BLOCKS = D // P
 HALF = 256
 HALVES = D // HALF
+MORE = 64
 
 FLOPS = 2 * P * D * (GATES * D) * OPERANDS
 
@@ -225,11 +226,13 @@ def tile_rlstmcell_pb_s_kernel(
             quantise((0, 1))
             multiply((0, 1))
             regroup(by_vector, (1, 0), 0)
-            regroup(by_scalar, (1, 1), 0)
+            regroup(by_vector, (1, 1), 0, 0, MORE)
+            regroup(by_scalar, (1, 1), 0, MORE, HALF - MORE)
             squash((0, 0))
             turn((0, 0))
             regroup(by_vector, (1, 0), 1)
-            regroup(by_scalar, (1, 1), 1)
+            regroup(by_vector, (1, 1), 1, 0, MORE)
+            regroup(by_scalar, (1, 1), 1, MORE, HALF - MORE)
             quantise((1, 0))
             multiply((1, 0))
             squash((0, 1))

@@ -34,7 +34,7 @@ def tile_rlstmcell_pb_s_kernel(
         consts = ctx.enter_context(tc.tile_pool(name="consts", bufs=1))
         wpool = ctx.enter_context(tc.tile_pool(name="wpool", bufs=GATES * HALVES + 1))
         psum_in = ctx.enter_context(tc.psum_pool(name="psum_in", bufs=1))
-        psum_gate = ctx.enter_context(tc.psum_pool(name="psum_gate", bufs=3))
+        psum_gate = ctx.enter_context(tc.psum_pool(name="psum_gate", bufs=4))
         psum_out = ctx.enter_context(tc.psum_pool(name="psum_out", bufs=3))
 
         raws = {}
@@ -102,7 +102,7 @@ def tile_rlstmcell_pb_s_kernel(
             )
 
         def transpose_bias():
-            bias_cols_ps = psum_in.tile([P, P], BF16)
+            bias_cols_ps = psum_out.tile([P, P], BF16, name="gate")
             nc.tensor.transpose(bias_cols_ps[:], bias_rows[:], ident_bf[:])
             nc.vector.tensor_copy(out=bias_cols[:], in_=bias_cols_ps[:, 0 : GATES * BLOCKS])
 
@@ -146,12 +146,13 @@ def tile_rlstmcell_pb_s_kernel(
 
         def multiply(piece):
             first, width = pieces[piece]
-            z = psum_gate.tile([P, width], F32)
+            sums_of[piece] = []
             for q in range(width // P):
                 block = slice(q * P, (q + 1) * P)
+                z = psum_gate.tile([P, P], F32)
                 for a in range(OPERANDS):
                     nc.tensor.matmul_mx(
-                        out=z[:, block],
+                        out=z[:],
                         lhsT=codes_of[piece][:, a, block].bitcast(FP8X4),
                         lhsT_scale=scales_of[piece][:, a, block],
                         rhs=xh_codes[:, a * P : (a + 1) * P].bitcast(FP8X4),
@@ -159,7 +160,7 @@ def tile_rlstmcell_pb_s_kernel(
                         start=(a == 0),
                         stop=(a == OPERANDS - 1),
                     )
-            sums_of[piece] = z
+                sums_of[piece].append(z)
 
         def squash(piece):
             first, width = pieces[piece]
@@ -169,7 +170,7 @@ def tile_rlstmcell_pb_s_kernel(
                 r = piece[0] * BLOCKS + first // P + q
                 nc.scalar.activation(
                     out=gate_t[:, block],
-                    in_=sums_of[piece][:, block],
+                    in_=sums_of[piece][q][:],
                     func=ACT.Sigmoid,
                     bias=bias_cols[:, r : r + 1],
                 )
@@ -239,7 +240,8 @@ def tile_rlstmcell_pb_s_kernel(
             quantise((1, 1))
             multiply((1, 1))
             turn((0, 1))
-            regroup(by_vector, (2, 0), 0)
+            regroup(by_vector, (2, 0), 0, 0, HALF - MORE)
+            regroup(by_scalar, (2, 0), 0, HALF - MORE, MORE)
             regroup(by_scalar, (2, 1), 0)
             regroup(by_scalar, (2, 2), 0)
             times_candidate(0)

@@ -17,9 +17,8 @@ D = 512
 GATES = 3
 OPERANDS = 2
 BLOCKS = D // P
-HALF = 256
-HALVES = D // HALF
-MORE = 64
+HALF = D // 2
+MOST = 320
 
 FLOPS = 2 * P * D * (GATES * D) * OPERANDS
 
@@ -29,28 +28,32 @@ def tile_rlstmcell_pb_s_kernel(
 ):
     nc = tc.nc
     weights = (kernel, recurrent_kernel)
+    gate_i, gate_f, gate_o = range(GATES)
+    by_x, by_h = range(OPERANDS)
 
     with ExitStack() as ctx:
         consts = ctx.enter_context(tc.tile_pool(name="consts", bufs=1))
-        wpool = ctx.enter_context(tc.tile_pool(name="wpool", bufs=GATES * HALVES + 1))
+        wpool = ctx.enter_context(tc.tile_pool(name="wpool", bufs=GATES * OPERANDS))
+        gpool = ctx.enter_context(tc.tile_pool(name="gpool", bufs=GATES * BLOCKS))
         psum_in = ctx.enter_context(tc.psum_pool(name="psum_in", bufs=1))
-        psum_gate = ctx.enter_context(tc.psum_pool(name="psum_gate", bufs=4))
+        psum_sum = ctx.enter_context(tc.psum_pool(name="psum_sum", bufs=4))
         psum_out = ctx.enter_context(tc.psum_pool(name="psum_out", bufs=3))
 
         raws = {}
 
-        def load_weight(g, a, first=0, width=D):
-            raw = wpool.tile([P, PACK, width], BF16)
-            at = g * D + first
-            nc.sync.dma_start(
-                out=raw[:],
-                in_=weights[a][:, at : at + width].rearrange("(p j) n -> p j n", j=PACK),
-            )
-            raws[g, a, first] = raw
-            if width == D:
-                raws[g, a, HALF] = raw[:, :, HALF:D]
+        def load_weight(g, a, parts=1):
+            raw = wpool.tile([P, PACK, D], BF16)
+            width = D // parts
+            for at in range(0, D, width):
+                nc.sync.dma_start(
+                    out=raw[:, :, at : at + width],
+                    in_=weights[a][:, g * D + at : g * D + at + width].rearrange(
+                        "(p j) n -> p j n", j=PACK
+                    ),
+                )
+            raws[g, a] = raw
 
-        load_weight(0, 0)
+        load_weight(gate_i, by_x)
         xh = consts.tile([P, OPERANDS, D], BF16)
         nc.sync.dma_start(out=xh[:, 0, :], in_=inputs)
         nc.sync.dma_start(out=xh[:, 1, :], in_=h_state)
@@ -59,14 +62,13 @@ def tile_rlstmcell_pb_s_kernel(
         nc.sync.dma_start(
             out=bias_rows[0 : GATES * BLOCKS, :], in_=bias.rearrange("(r c) -> r c", c=P)
         )
-        load_weight(0, 1)
+        load_weight(gate_i, by_h)
         cell_in = consts.tile([P, 2, D], BF16)
         nc.sync.dma_start(out=cell_in[:, 0, :], in_=c_upd.rearrange("b s d -> b (s d)"))
-        load_weight(1, 0)
-        load_weight(1, 1)
-        load_weight(2, 0)
-        load_weight(2, 1, 0, HALF)
-        load_weight(2, 1, HALF, HALF)
+        load_weight(gate_f, by_x)
+        load_weight(gate_f, by_h)
+        load_weight(gate_o, by_x)
+        load_weight(gate_o, by_h, parts=2)
         nc.sync.dma_start(out=cell_in[:, 1, :], in_=c_state)
 
         ident_f32 = consts.tile([P, P], F32)
@@ -88,7 +90,7 @@ def tile_rlstmcell_pb_s_kernel(
         i_cand = consts.tile([P, D], F32)
         f_c = consts.tile([P, D], F32)
 
-        def transpose_inputs():
+        def regroup_inputs():
             xh_words = xh[:].rearrange("b a k -> b (a k)").bitcast(F32).rearrange(
                 "b (a p u) -> b a u p", a=OPERANDS, u=2
             )
@@ -101,7 +103,12 @@ def tile_rlstmcell_pb_s_kernel(
                 in_=xh_t[:].rearrange("p a u b -> p a b u"),
             )
 
-        def transpose_bias():
+        def quantise_inputs():
+            nc.vector.quantize_mx(
+                out=xh_codes[:].bitcast(FP8X4), scales=xh_scales[:], in_=xh_grouped[:]
+            )
+
+        def turn_bias():
             bias_cols_ps = psum_out.tile([P, P], BF16, name="gate")
             nc.tensor.transpose(bias_cols_ps[:], bias_rows[:], ident_bf[:])
             nc.vector.tensor_copy(out=bias_cols[:], in_=bias_cols_ps[:, 0 : GATES * BLOCKS])
@@ -109,169 +116,141 @@ def tile_rlstmcell_pb_s_kernel(
         def candidate():
             nc.scalar.activation(out=cand[:], in_=cell_in[:, 0, :], func=ACT.Tanh)
 
-        def quantise_inputs():
-            nc.vector.quantize_mx(
-                out=xh_codes[:].bitcast(FP8X4), scales=xh_scales[:], in_=xh_grouped[:]
-            )
+        groupeds, codes_of, scales_of, sums_of, gates_t, gates = {}, {}, {}, {}, {}, {}
+        for g in range(GATES):
+            for a in range(OPERANDS):
+                grouped = wpool.tile([P, D, PACK], BF16, align_bytes=64)
+                codes = wpool.tile([P, D], U32, align_bytes=64)
+                scales = wpool.tile([P, D], U8, align_bytes=64)
+                groupeds[g, a], codes_of[g, a], scales_of[g, a] = grouped, codes, scales
 
-        pieces = {(g, s): (s * HALF, HALF) for g in range(GATES) for s in range(HALVES)}
-        pieces[2, 1] = (HALF, P)
-        pieces[2, 2] = (HALF + P, P)
-        groupeds, codes_of, scales_of, sums_of, turned_of, gates_of = {}, {}, {}, {}, {}, {}
-        for piece, (first, width) in pieces.items():
-            grouped = wpool.tile([P, OPERANDS, width, PACK], BF16, align_bytes=64)
-            groupeds[piece] = grouped
-
-        def regroup(copy, piece, a, at=0, width=None):
-            first, whole = pieces[piece]
-            width = width or whole
-            half = first // HALF * HALF
-            raw = raws[piece[0], a, half]
-            col = first - half + at
+        def regroup(copy, g, a, lo, hi):
             copy(
-                out=groupeds[piece][:, a, at : at + width, :].rearrange("p (c i) j -> p c j i", i=4),
-                in_=raw[:, :, col : col + width].rearrange("p j (c i) -> p c j i", i=4),
+                out=groupeds[g, a][:, lo:hi, :].rearrange("p (c i) j -> p c j i", i=4),
+                in_=raws[g, a][:, :, lo:hi].rearrange("p j (c i) -> p c j i", i=4),
             )
 
-        def quantise(piece):
-            first, width = pieces[piece]
-            codes = wpool.tile([P, OPERANDS, width], U32, align_bytes=64)
-            scales = wpool.tile([P, OPERANDS, width], U8, align_bytes=64)
+        def by_vector(g, a, lo, hi):
+            regroup(nc.vector.tensor_copy, g, a, lo, hi)
+
+        def by_scalar(g, a, lo, hi):
+            regroup(nc.scalar.copy, g, a, lo, hi)
+
+        def quantise(g, a, lo, hi):
             nc.vector.quantize_mx(
-                out=codes[:].rearrange("p a n -> p (a n)").bitcast(FP8X4),
-                scales=scales[:].rearrange("p a n -> p (a n)"),
-                in_=groupeds[piece][:].rearrange("p a n j -> p (a n j)"),
+                out=codes_of[g, a][:, lo:hi].bitcast(FP8X4),
+                scales=scales_of[g, a][:, lo:hi],
+                in_=groupeds[g, a][:, lo:hi, :].rearrange("p n j -> p (n j)"),
             )
-            codes_of[piece], scales_of[piece] = codes, scales
 
-        def multiply(piece):
-            first, width = pieces[piece]
-            sums_of[piece] = []
-            for q in range(width // P):
-                block = slice(q * P, (q + 1) * P)
-                z = psum_gate.tile([P, P], F32)
+        def multiply(g, lo, hi):
+            for at in range(lo, hi, P):
+                z = psum_sum.tile([P, P], F32)
                 for a in range(OPERANDS):
                     nc.tensor.matmul_mx(
                         out=z[:],
-                        lhsT=codes_of[piece][:, a, block].bitcast(FP8X4),
-                        lhsT_scale=scales_of[piece][:, a, block],
+                        lhsT=codes_of[g, a][:, at : at + P].bitcast(FP8X4),
+                        lhsT_scale=scales_of[g, a][:, at : at + P],
                         rhs=xh_codes[:, a * P : (a + 1) * P].bitcast(FP8X4),
                         rhs_scale=xh_scales[:, a * P : (a + 1) * P],
                         start=(a == 0),
                         stop=(a == OPERANDS - 1),
                     )
-                sums_of[piece].append(z)
+                sums_of[g, at] = z
 
-        def squash(piece):
-            first, width = pieces[piece]
-            gate_t = wpool.tile([P, width], F32)
-            for q in range(width // P):
-                block = slice(q * P, (q + 1) * P)
-                r = piece[0] * BLOCKS + first // P + q
+        def squash(g, lo, hi):
+            for at in range(lo, hi, P):
+                r = g * BLOCKS + at // P
+                gate_t = gpool.tile([P, P], F32)
                 nc.scalar.activation(
-                    out=gate_t[:, block],
-                    in_=sums_of[piece][q][:],
-                    func=ACT.Sigmoid,
-                    bias=bias_cols[:, r : r + 1],
+                    out=gate_t[:], in_=sums_of[g, at][:], func=ACT.Sigmoid, bias=bias_cols[:, r : r + 1]
                 )
-            turned_of[piece] = gate_t
+                gates_t[g, at] = gate_t
 
-        def turn(piece):
-            first, width = pieces[piece]
-            gate_t = turned_of[piece]
-            gate = psum_out.tile([P, width], F32)
-            for q in range(width // P):
-                block = slice(q * P, (q + 1) * P)
-                nc.tensor.transpose(gate[:, block], gate_t[:, block], ident_f32[:])
-            gates_of[piece] = gate
+        def turn(g, lo, hi):
+            gate = psum_out.tile([P, hi - lo], F32)
+            for at in range(lo, hi, P):
+                nc.tensor.transpose(gate[:, at - lo : at - lo + P], gates_t[g, at][:], ident_f32[:])
+            gates[g, lo] = gate
 
-        def columns(piece):
-            first, width = pieces[piece]
-            return slice(first, first + width)
+        def times_candidate(lo, hi):
+            nc.vector.tensor_mul(out=i_cand[:, lo:hi], in0=gates[gate_i, lo][:], in1=cand[:, lo:hi])
 
-        def times_candidate(s):
-            cols = columns((0, s))
-            nc.vector.tensor_mul(out=i_cand[:, cols], in0=gates_of[0, s][:], in1=cand[:, cols])
+        def times_cell(lo, hi):
+            nc.vector.tensor_mul(out=f_c[:, lo:hi], in0=gates[gate_f, lo][:], in1=cell_in[:, 1, lo:hi])
 
-        def times_cell(s):
-            cols = columns((1, s))
-            nc.vector.tensor_mul(out=f_c[:, cols], in0=gates_of[1, s][:], in1=cell_in[:, 1, cols])
+        def new_cell(lo, hi):
+            nc.vector.tensor_add(out=c_new[:, lo:hi], in0=f_c[:, lo:hi], in1=i_cand[:, lo:hi])
+            nc.sync.dma_start(out=out_1[:, lo:hi], in_=c_new[:, lo:hi])
 
-        def new_cell(s):
-            cols = columns((1, s))
-            nc.vector.tensor_add(out=c_new[:, cols], in0=f_c[:, cols], in1=i_cand[:, cols])
-            nc.sync.dma_start(out=out_1[:, cols], in_=c_new[:, cols])
+        def tanh_of_cell(lo, hi):
+            nc.scalar.activation(out=tanh_c[:, lo:hi], in_=c_new[:, lo:hi], func=ACT.Tanh)
 
-        def tanh_of_cell(s):
-            cols = columns((1, s))
-            nc.scalar.activation(out=tanh_c[:, cols], in_=c_new[:, cols], func=ACT.Tanh)
+        def new_hidden(lo, hi):
+            nc.vector.tensor_mul(out=h_new[:, lo:hi], in0=gates[gate_o, lo][:], in1=tanh_c[:, lo:hi])
+            nc.sync.dma_start(out=out_0[:, lo:hi], in_=h_new[:, lo:hi])
 
-        def new_hidden(s):
-            cols = columns((2, s))
-            nc.vector.tensor_mul(out=h_new[:, cols], in0=gates_of[2, s][:], in1=tanh_c[:, cols])
-            nc.sync.dma_start(out=out_0[:, cols], in_=h_new[:, cols])
-
-        by_vector, by_scalar = nc.vector.tensor_copy, nc.scalar.copy
+        left, right = (0, HALF), (HALF, D)
+        third, fourth = (HALF, HALF + P), (HALF + P, D)
 
         with tc.manual_schedule(engines={ENGINE.DVE, ENGINE.Activation, ENGINE.PE}):
-            regroup(by_vector, (0, 0), 0)
-            regroup(by_scalar, (0, 1), 0)
-            transpose_inputs()
-            regroup(by_vector, (0, 0), 1)
-            regroup(by_scalar, (0, 1), 1)
-            transpose_bias()
+            by_vector(gate_i, by_x, 0, HALF)
+            by_scalar(gate_i, by_x, HALF, D)
+            regroup_inputs()
+            quantise(gate_i, by_x, 0, D)
+            by_vector(gate_i, by_h, 0, MOST)
+            by_scalar(gate_i, by_h, MOST, D)
+            turn_bias()
             candidate()
             quantise_inputs()
-            quantise((0, 0))
-            multiply((0, 0))
-            quantise((0, 1))
-            multiply((0, 1))
-            regroup(by_vector, (1, 0), 0)
-            regroup(by_vector, (1, 1), 0, 0, MORE)
-            regroup(by_scalar, (1, 1), 0, MORE, HALF - MORE)
-            squash((0, 0))
-            turn((0, 0))
-            regroup(by_vector, (1, 0), 1)
-            regroup(by_vector, (1, 1), 1, 0, MORE)
-            regroup(by_scalar, (1, 1), 1, MORE, HALF - MORE)
-            quantise((1, 0))
-            multiply((1, 0))
-            squash((0, 1))
-            quantise((1, 1))
-            multiply((1, 1))
-            turn((0, 1))
-            regroup(by_vector, (2, 0), 0, 0, HALF - MORE)
-            regroup(by_scalar, (2, 0), 0, HALF - MORE, MORE)
-            regroup(by_scalar, (2, 1), 0)
-            regroup(by_scalar, (2, 2), 0)
-            times_candidate(0)
-            regroup(by_vector, (2, 0), 1, 0, P)
-            regroup(by_scalar, (2, 0), 1, P, P)
-            squash((1, 0))
-            turn((1, 0))
-            squash((1, 1))
-            turn((1, 1))
-            regroup(by_vector, (2, 1), 1)
-            regroup(by_scalar, (2, 2), 1)
-            quantise((2, 0))
-            multiply((2, 0))
-            quantise((2, 1))
-            multiply((2, 1))
-            times_candidate(1)
-            quantise((2, 2))
-            multiply((2, 2))
-            times_cell(0)
-            times_cell(1)
-            new_cell(0)
-            new_cell(1)
-            squash((2, 0))
-            turn((2, 0))
-            squash((2, 1))
-            squash((2, 2))
-            tanh_of_cell(0)
-            tanh_of_cell(1)
-            turn((2, 1))
-            turn((2, 2))
-            new_hidden(0)
-            new_hidden(1)
-            new_hidden(2)
+            quantise(gate_i, by_h, *left)
+            multiply(gate_i, *left)
+            quantise(gate_i, by_h, *right)
+            multiply(gate_i, *right)
+            by_vector(gate_f, by_x, 0, MOST)
+            by_scalar(gate_f, by_x, MOST, D)
+            squash(gate_i, *left)
+            turn(gate_i, *left)
+            quantise(gate_f, by_x, 0, D)
+            by_vector(gate_f, by_h, 0, HALF)
+            by_scalar(gate_f, by_h, HALF, D)
+            times_candidate(*left)
+            quantise(gate_f, by_h, *left)
+            multiply(gate_f, *left)
+            squash(gate_i, *right)
+            quantise(gate_f, by_h, *right)
+            multiply(gate_f, *right)
+            turn(gate_i, *right)
+            by_vector(gate_o, by_x, 0, HALF)
+            by_scalar(gate_o, by_x, HALF, D)
+            by_vector(gate_o, by_h, 0, HALF - P // 2)
+            by_scalar(gate_o, by_h, HALF - P // 2, HALF)
+            squash(gate_f, *left)
+            turn(gate_f, *left)
+            squash(gate_f, *right)
+            turn(gate_f, *right)
+            quantise(gate_o, by_x, 0, D)
+            quantise(gate_o, by_h, *left)
+            multiply(gate_o, *left)
+            by_vector(gate_o, by_h, *third)
+            by_scalar(gate_o, by_h, *fourth)
+            times_candidate(*right)
+            quantise(gate_o, by_h, *third)
+            multiply(gate_o, *third)
+            quantise(gate_o, by_h, *fourth)
+            multiply(gate_o, *fourth)
+            times_cell(*left)
+            times_cell(*right)
+            new_cell(*left)
+            new_cell(*right)
+            squash(gate_o, *left)
+            turn(gate_o, *left)
+            squash(gate_o, *third)
+            squash(gate_o, *fourth)
+            tanh_of_cell(*left)
+            tanh_of_cell(*right)
+            turn(gate_o, *third)
+            turn(gate_o, *fourth)
+            new_hidden(*left)
+            new_hidden(*third)
+            new_hidden(*fourth)

@@ -171,13 +171,15 @@ def tile_rlstmcell_pb_s_kernel(
             gate = psum_out.tile([P, hi - lo], F32)
             for at in range(lo, hi, P):
                 nc.tensor.transpose(gate[:, at - lo : at - lo + P], gates_t[g, at][:], ident_f32[:])
-            gates[g, lo] = gate
+            for at in range(lo, hi, P):
+                gates[g, at] = gate[:, at - lo : at - lo + P]
+            gates[g, lo] = gate[:]
 
         def times_candidate(lo, hi):
-            nc.vector.tensor_mul(out=i_cand[:, lo:hi], in0=gates[gate_i, lo][:], in1=cand[:, lo:hi])
+            nc.vector.tensor_mul(out=i_cand[:, lo:hi], in0=gates[gate_i, lo], in1=cand[:, lo:hi])
 
         def times_cell(lo, hi):
-            nc.vector.tensor_mul(out=f_c[:, lo:hi], in0=gates[gate_f, lo][:], in1=cell_in[:, 1, lo:hi])
+            nc.vector.tensor_mul(out=f_c[:, lo:hi], in0=gates[gate_f, lo][:, 0 : hi - lo], in1=cell_in[:, 1, lo:hi])
 
         def new_cell(lo, hi):
             nc.vector.tensor_add(out=c_new[:, lo:hi], in0=f_c[:, lo:hi], in1=i_cand[:, lo:hi])
@@ -187,7 +189,7 @@ def tile_rlstmcell_pb_s_kernel(
             nc.scalar.activation(out=tanh_c[:, lo:hi], in_=c_new[:, lo:hi], func=ACT.Tanh)
 
         def new_hidden(lo, hi):
-            nc.vector.tensor_mul(out=h_new[:, lo:hi], in0=gates[gate_o, lo][:], in1=tanh_c[:, lo:hi])
+            nc.vector.tensor_mul(out=h_new[:, lo:hi], in0=gates[gate_o, lo], in1=tanh_c[:, lo:hi])
             nc.sync.dma_start(out=out_0[:, lo:hi], in_=h_new[:, lo:hi])
 
         left, right = (0, HALF), (HALF, D)
@@ -237,18 +239,21 @@ def tile_rlstmcell_pb_s_kernel(
             times_candidate(*right)
             quantise(gate_o, by_h, *third)
             multiply(gate_o, *third)
+            times_cell(*left)
             quantise(gate_o, by_h, *fourth)
             multiply(gate_o, *fourth)
-            times_cell(*left)
-            times_cell(*right)
             new_cell(*left)
-            new_cell(*right)
+            times_cell(*third)
+            times_cell(*fourth)
+            new_cell(*third)
+            new_cell(*fourth)
             squash(gate_o, *left)
             turn(gate_o, *left)
             squash(gate_o, *third)
-            squash(gate_o, *fourth)
             tanh_of_cell(*left)
-            tanh_of_cell(*right)
+            squash(gate_o, *fourth)
+            tanh_of_cell(*third)
+            tanh_of_cell(*fourth)
             turn(gate_o, *third)
             turn(gate_o, *fourth)
             new_hidden(*left)

@@ -59,9 +59,9 @@ def tile_rlstmcell_pb_s_kernel(
         nc.sync.dma_start(out=xh[:, 1, :], in_=h_state)
         bias_rows = consts.tile([P, P], BF16)
         nc.vector.memset(bias_rows[:], 0.0)
-        nc.sync.dma_start(
-            out=bias_rows[0 : GATES * BLOCKS, :], in_=bias.rearrange("(r c) -> r c", c=P)
-        )
+        bias_by_block = bias.rearrange("(r c) -> r c", c=P)
+        for lo, hi in ((0, 8), (8, GATES * BLOCKS)):
+            nc.sync.dma_start(out=bias_rows[lo:hi, :], in_=bias_by_block[lo:hi, :])
         load_weight(gate_i, by_h)
         cell_in = consts.tile([P, 2, D], BF16)
         nc.sync.dma_start(out=cell_in[:, 0, :], in_=c_upd.rearrange("b s d -> b (s d)"))
@@ -111,7 +111,7 @@ def tile_rlstmcell_pb_s_kernel(
         def turn_bias():
             bias_cols_ps = psum_out.tile([P, P], BF16, name="gate")
             nc.tensor.transpose(bias_cols_ps[:], bias_rows[:], ident_bf[:])
-            nc.vector.tensor_copy(out=bias_cols[:], in_=bias_cols_ps[:, 0 : GATES * BLOCKS])
+            nc.scalar.copy(out=bias_cols[:], in_=bias_cols_ps[:, 0 : GATES * BLOCKS])
 
         def candidate():
             nc.scalar.activation(out=cand[:], in_=cell_in[:, 0, :], func=ACT.Tanh)
@@ -202,8 +202,8 @@ def tile_rlstmcell_pb_s_kernel(
             quantise(gate_i, by_x, 0, D)
             by_vector(gate_i, by_h, 0, MOST)
             by_scalar(gate_i, by_h, MOST, D)
-            turn_bias()
             candidate()
+            turn_bias()
             quantise_inputs()
             quantise(gate_i, by_h, *left)
             multiply(gate_i, *left)

from contextlib import ExitStack

import concourse.mybir as mybir
from concourse.masks import make_identity

F32 = mybir.dt.float32
BF16 = mybir.dt.bfloat16
U32 = mybir.dt.uint32
U8 = mybir.dt.uint8
FP8X4 = mybir.dt.float8_e4m3fn_x4
ACT = mybir.ActivationFunctionType
ENGINE = mybir.EngineType

P = 128
PACK = 4
D = 512
GATES = 3
OPERANDS = 2
BLOCKS = D // P
HALF = D // 2
MOST = 320

FLOPS = 2 * P * D * (GATES * D) * OPERANDS


def tile_rlstmcell_pb_s_kernel(
    tc, inputs, h_state, c_state, c_upd, kernel, recurrent_kernel, bias, out_0, out_1
):
    nc = tc.nc
    weights = (kernel, recurrent_kernel)
    gate_i, gate_f, gate_o = range(GATES)
    by_x, by_h = range(OPERANDS)

    with ExitStack() as ctx:
        consts = ctx.enter_context(tc.tile_pool(name="consts", bufs=1))
        wpool = ctx.enter_context(tc.tile_pool(name="wpool", bufs=GATES * OPERANDS))
        gpool = ctx.enter_context(tc.tile_pool(name="gpool", bufs=GATES * BLOCKS))
        psum_in = ctx.enter_context(tc.psum_pool(name="psum_in", bufs=1))
        psum_sum = ctx.enter_context(tc.psum_pool(name="psum_sum", bufs=4))
        psum_out = ctx.enter_context(tc.psum_pool(name="psum_out", bufs=3))

        raws = {}

        def load_weight(g, a, parts=1):
            raw = wpool.tile([P, PACK, D], BF16)
            width = D // parts
            for at in range(0, D, width):
                nc.sync.dma_start(
                    out=raw[:, :, at : at + width],
                    in_=weights[a][:, g * D + at : g * D + at + width].rearrange(
                        "(p j) n -> p j n", j=PACK
                    ),
                )
            raws[g, a] = raw

        load_weight(gate_i, by_x)
        xh = consts.tile([P, OPERANDS, D], BF16)
        nc.sync.dma_start(out=xh[:, 0, :], in_=inputs)
        nc.sync.dma_start(out=xh[:, 1, :], in_=h_state)
        bias_rows = consts.tile([P, P], BF16)
        nc.vector.memset(bias_rows[:], 0.0)
        bias_by_block = bias.rearrange("(r c) -> r c", c=P)
        for lo, hi in ((0, 8), (8, GATES * BLOCKS)):
            nc.sync.dma_start(out=bias_rows[lo:hi, :], in_=bias_by_block[lo:hi, :])
        load_weight(gate_i, by_h)
        cell_in = consts.tile([P, 2, D], BF16)
        nc.sync.dma_start(out=cell_in[:, 0, :], in_=c_upd.rearrange("b s d -> b (s d)"))
        load_weight(gate_f, by_x)
        load_weight(gate_f, by_h)
        load_weight(gate_o, by_x)
        load_weight(gate_o, by_h, parts=2)
        nc.sync.dma_start(out=cell_in[:, 1, :], in_=c_state)

        ident_f32 = consts.tile([P, P], F32)
        make_identity(nc, ident_f32[:])
        ident_bf = consts.tile([P, P], BF16)
        make_identity(nc, ident_bf[:])
        warm = consts.tile([P, 1], F32)
        nc.vector.memset(warm[:], 0.0)
        nc.scalar.activation(out=warm[:], in_=warm[:], func=ACT.Sigmoid)

        bias_cols = consts.tile([P, GATES * BLOCKS], F32)
        xh_grouped = consts.tile([P, OPERANDS * P * PACK], BF16, align_bytes=64)
        xh_codes = consts.tile([P, OPERANDS * P], U32, align_bytes=64)
        xh_scales = consts.tile([P, OPERANDS * P], U8, align_bytes=64)
        cand = consts.tile([P, D], F32)
        c_new = consts.tile([P, D], F32)
        tanh_c = consts.tile([P, D], F32)
        h_new = consts.tile([P, D], F32)
        i_cand = consts.tile([P, D], F32)
        f_c = consts.tile([P, D], F32)

        def regroup_inputs():
            xh_words = xh[:].rearrange("b a k -> b (a k)").bitcast(F32).rearrange(
                "b (a p u) -> b a u p", a=OPERANDS, u=2
            )
            xh_t = psum_in.tile([P, OPERANDS, 2, P], F32)
            for a in range(OPERANDS):
                for u in range(2):
                    nc.tensor.transpose(xh_t[:, a, u, :], xh_words[:, a, u, :], ident_f32[:])
            nc.scalar.copy(
                out=xh_grouped[:].bitcast(F32).rearrange("p (a b u) -> p a b u", a=OPERANDS, u=2),
                in_=xh_t[:].rearrange("p a u b -> p a b u"),
            )

        def quantise_inputs():
            nc.vector.quantize_mx(
                out=xh_codes[:].bitcast(FP8X4), scales=xh_scales[:], in_=xh_grouped[:]
            )

        def turn_bias():
            bias_cols_ps = psum_out.tile([P, P], BF16, name="gate")
            nc.tensor.transpose(bias_cols_ps[:], bias_rows[:], ident_bf[:])
            nc.scalar.copy(out=bias_cols[:], in_=bias_cols_ps[:, 0 : GATES * BLOCKS])

        def candidate():
            nc.scalar.activation(out=cand[:], in_=cell_in[:, 0, :], func=ACT.Tanh)

        groupeds, codes_of, scales_of, sums_of, gates_t, gates = {}, {}, {}, {}, {}, {}
        for g in range(GATES):
            for a in range(OPERANDS):
                grouped = wpool.tile([P, D, PACK], BF16, align_bytes=64)
                codes = wpool.tile([P, D], U32, align_bytes=64)
                scales = wpool.tile([P, D], U8, align_bytes=64)
                groupeds[g, a], codes_of[g, a], scales_of[g, a] = grouped, codes, scales

        def regroup(copy, g, a, lo, hi):
            copy(
                out=groupeds[g, a][:, lo:hi, :].rearrange("p (c i) j -> p c j i", i=4),
                in_=raws[g, a][:, :, lo:hi].rearrange("p j (c i) -> p c j i", i=4),
            )

        def by_vector(g, a, lo, hi):
            regroup(nc.vector.tensor_copy, g, a, lo, hi)

        def by_scalar(g, a, lo, hi):
            regroup(nc.scalar.copy, g, a, lo, hi)

        def quantise(g, a, lo, hi):
            nc.vector.quantize_mx(
                out=codes_of[g, a][:, lo:hi].bitcast(FP8X4),
                scales=scales_of[g, a][:, lo:hi],
                in_=groupeds[g, a][:, lo:hi, :].rearrange("p n j -> p (n j)"),
            )

        def multiply(g, lo, hi):
            for at in range(lo, hi, P):
                z = psum_sum.tile([P, P], F32)
                for a in range(OPERANDS):
                    nc.tensor.matmul_mx(
                        out=z[:],
                        lhsT=codes_of[g, a][:, at : at + P].bitcast(FP8X4),
                        lhsT_scale=scales_of[g, a][:, at : at + P],
                        rhs=xh_codes[:, a * P : (a + 1) * P].bitcast(FP8X4),
                        rhs_scale=xh_scales[:, a * P : (a + 1) * P],
                        start=(a == 0),
                        stop=(a == OPERANDS - 1),
                    )
                sums_of[g, at] = z

        def squash(g, lo, hi):
            for at in range(lo, hi, P):
                r = g * BLOCKS + at // P
                gate_t = gpool.tile([P, P], F32)
                nc.scalar.activation(
                    out=gate_t[:], in_=sums_of[g, at][:], func=ACT.Sigmoid, bias=bias_cols[:, r : r + 1]
                )
                gates_t[g, at] = gate_t

        def turn(g, lo, hi):
            gate = psum_out.tile([P, hi - lo], F32)
            for at in range(lo, hi, P):
                nc.tensor.transpose(gate[:, at - lo : at - lo + P], gates_t[g, at][:], ident_f32[:])
            for at in range(lo, hi, P):
                gates[g, at] = gate[:, at - lo : at - lo + P]
            gates[g, lo] = gate[:]

        def times_candidate(lo, hi):
            nc.vector.tensor_mul(out=i_cand[:, lo:hi], in0=gates[gate_i, lo], in1=cand[:, lo:hi])

        def times_cell(lo, hi):
            nc.vector.tensor_mul(out=f_c[:, lo:hi], in0=gates[gate_f, lo][:, 0 : hi - lo], in1=cell_in[:, 1, lo:hi])

        def new_cell(lo, hi):
            nc.vector.tensor_add(out=c_new[:, lo:hi], in0=f_c[:, lo:hi], in1=i_cand[:, lo:hi])
            nc.sync.dma_start(out=out_1[:, lo:hi], in_=c_new[:, lo:hi])

        def tanh_of_cell(lo, hi):
            nc.scalar.activation(out=tanh_c[:, lo:hi], in_=c_new[:, lo:hi], func=ACT.Tanh)

        def new_hidden(lo, hi):
            nc.vector.tensor_mul(out=h_new[:, lo:hi], in0=gates[gate_o, lo], in1=tanh_c[:, lo:hi])
            nc.sync.dma_start(out=out_0[:, lo:hi], in_=h_new[:, lo:hi])

        left, right = (0, HALF), (HALF, D)
        third, fourth = (HALF, HALF + P), (HALF + P, D)

        with tc.manual_schedule(engines={ENGINE.DVE, ENGINE.Activation, ENGINE.PE}):
            by_vector(gate_i, by_x, 0, HALF)
            by_scalar(gate_i, by_x, HALF, D)
            regroup_inputs()
            quantise(gate_i, by_x, 0, D)
            by_vector(gate_i, by_h, 0, MOST)
            by_scalar(gate_i, by_h, MOST, D)
            candidate()
            turn_bias()
            quantise_inputs()
            quantise(gate_i, by_h, *left)
            multiply(gate_i, *left)
            quantise(gate_i, by_h, *right)
            multiply(gate_i, *right)
            by_vector(gate_f, by_x, 0, MOST)
            by_scalar(gate_f, by_x, MOST, D)
            squash(gate_i, *left)
            turn(gate_i, *left)
            quantise(gate_f, by_x, 0, D)
            by_vector(gate_f, by_h, 0, HALF)
            by_scalar(gate_f, by_h, HALF, D)
            times_candidate(*left)
            quantise(gate_f, by_h, *left)
            multiply(gate_f, *left)
            squash(gate_i, *right)
            quantise(gate_f, by_h, *right)
            multiply(gate_f, *right)
            turn(gate_i, *right)
            by_vector(gate_o, by_x, 0, HALF)
            by_scalar(gate_o, by_x, HALF, D)
            by_vector(gate_o, by_h, 0, HALF - P // 2)
            by_scalar(gate_o, by_h, HALF - P // 2, HALF)
            squash(gate_f, *left)
            turn(gate_f, *left)
            squash(gate_f, *right)
            turn(gate_f, *right)
            quantise(gate_o, by_x, 0, D)
            quantise(gate_o, by_h, *left)
            multiply(gate_o, *left)
            by_vector(gate_o, by_h, *third)
            by_scalar(gate_o, by_h, *fourth)
            times_candidate(*right)
            quantise(gate_o, by_h, *third)
            multiply(gate_o, *third)
            times_cell(*left)
            quantise(gate_o, by_h, *fourth)
            multiply(gate_o, *fourth)
            new_cell(*left)
            times_cell(*third)
            times_cell(*fourth)
            new_cell(*third)
            new_cell(*fourth)
            squash(gate_o, *left)
            turn(gate_o, *left)
            squash(gate_o, *third)
            tanh_of_cell(*left)
            squash(gate_o, *fourth)
            tanh_of_cell(*third)
            tanh_of_cell(*fourth)
            turn(gate_o, *third)
            turn(gate_o, *fourth)
            new_hidden(*left)
            new_hidden(*third)
            new_hidden(*fourth)
